import numpy as np
import ml_dtypes


def mxq(x, axis, fmt="e4m3"):
    dtype, down = {"e4m3": (ml_dtypes.float8_e4m3fn, 7), "e5m2": (ml_dtypes.float8_e5m2, 14)}[fmt]
    v = np.moveaxis(np.asarray(x, np.float32).astype(ml_dtypes.bfloat16).astype(np.float64), axis, -1)
    blocks = v.reshape(v.shape[:-1] + (-1, 32))
    amax = np.abs(blocks).max(-1, keepdims=True)
    byte = np.maximum(np.where(amax > 0, np.frexp(amax)[1] - 1 + 127, 0) - down, 1)
    scale = np.exp2(byte - 127.0)
    codes = (blocks / scale).astype(np.float32).astype(dtype).astype(np.float64)
    return np.moveaxis((codes * scale).reshape(v.shape), -1, axis)


WIDE = False


def mx_kscale(k):
    if not WIDE:
        return np.ones(k)
    levels = np.array([10, -10, 5, -5, 0])
    a = np.random.permutation(np.resize(levels, k // 512 * 4)).reshape(k // 512, 4)
    idx = np.arange(k)
    return np.exp2(a[idx // 512, idx % 128 // 32])


BF16 = ml_dtypes.bfloat16


def bf(x):
    return np.asarray(x, np.float32).astype(BF16)


def f64(x):
    return np.asarray(x).astype(np.float64)


B, CH, CQ, CV, H, W = 4, 512, 128, 256, 32, 64
EPS = 1e-5
POOL = 2
HW = H * W
HW4 = HW // (POOL * POOL)
A = 1.5 / CQ ** 0.25


def bn(y, s, b, m, v):
    inv = f64(s) / np.sqrt(f64(v) + EPS)
    return y * inv[None, :, None] + (f64(b) - f64(m) * inv)[None, :, None]


def maxpool(y):
    c = y.shape[1]
    return y.reshape(B, c, H // POOL, POOL, W // POOL, POOL).max(axis=(3, 5)).reshape(B, c, HW4)


def vec(c, z):
    return bf(z * np.random.standard_normal(c))


def pos(c):
    return bf(0.5 + np.random.random(c))


def setup_inputs():
    s = mx_kscale(CH)
    return {'memory': bf(np.random.standard_normal((B, CH, H, W)) * s[None, :, None, None]),
            'wq': bf(np.random.standard_normal((CQ, CH)) * A / np.sqrt(CH) / s), 'bq': vec(CQ, 0.1),
            'bnq_s': pos(CQ), 'bnq_b': vec(CQ, 0.1), 'bnq_m': vec(CQ, 0.1), 'bnq_v': pos(CQ),
            'wk': bf(np.random.standard_normal((CQ, CH)) * A / np.sqrt(CH) / s), 'bk': vec(CQ, 0.1),
            'bnk_s': pos(CQ), 'bnk_b': vec(CQ, 0.1), 'bnk_m': vec(CQ, 0.1), 'bnk_v': pos(CQ),
            'wv': bf(np.random.standard_normal((CV, CH)) / np.sqrt(CH) / s), 'bv': vec(CV, 0.3),
            'bnv_s': pos(CV), 'bnv_b': vec(CV, 0.3), 'bnv_m': vec(CV, 0.3), 'bnv_v': pos(CV)}


def reference(memory, wq, bq, bnq_s, bnq_b, bnq_m, bnq_v, wk, bk, bnk_s, bnk_b, bnk_m, bnk_v, wv, bv, bnv_s, bnv_b, bnv_m, bnv_v):
    mq = mxq(f64(memory).reshape(B, CH, HW), 1, 'e4m3')
    yq = (mxq(f64(wq), 1, 'e4m3') @ mq) + f64(bq)[None, :, None]
    yk = (mxq(f64(wk), 1, 'e4m3') @ mq) + f64(bk)[None, :, None]
    yv = (mxq(f64(wv), 1, 'e4m3') @ mq) + f64(bv)[None, :, None]
    q = bn(yq, bnq_s, bnq_b, bnq_m, bnq_v).transpose(0, 2, 1)
    k = maxpool(bn(yk, bnk_s, bnk_b, bnk_m, bnk_v))
    v = maxpool(bn(yv, bnv_s, bnv_b, bnv_m, bnv_v)).transpose(0, 2, 1)
    return q, k, v

@@ -1,0 +1,309 @@
+from contextlib import ExitStack
+
+import concourse.mybir as mybir
+from concourse.masks import make_identity
+
+F32 = mybir.dt.float32
+BF16 = mybir.dt.bfloat16
+U32 = mybir.dt.uint32
+U8 = mybir.dt.uint8
+FP8X4 = mybir.dt.float8_e4m3fn_x4
+ACT = mybir.ActivationFunctionType
+ALU = mybir.AluOpType
+
+IMAGES = 4
+CHANNELS = 512
+WIDTH = 64
+POSITIONS = 2048
+EPS = 1e-5
+
+P = 128
+PACK = 4
+UNIT = 512
+UNITS_PER_IMAGE = POSITIONS // UNIT
+UNITS = IMAGES * UNITS_PER_IMAGE
+POOLED = UNIT // 4
+RUN = 4
+
+GROUPS = 4
+GROUP_Q = 0
+GROUP_K = 1
+POOLED_GROUPS = (1, 2, 3)
+
+KINDS = 5
+BIAS = 0
+GAIN = 1
+SHIFT = 2
+MEAN = 3
+VARIANCE = 4
+
+VECTOR_RUNS = 80
+LEAD = 5
+
+SMALL_LOADS_PER_LARGE = 3
+
+FLOPS = 2 * IMAGES * POSITIONS * CHANNELS * GROUPS * P
+
+
+def tile_selfattention_pa_t_kernel(
+    tc,
+    memory,
+    wq, bq, bnq_s, bnq_b, bnq_m, bnq_v,
+    wk, bk, bnk_s, bnk_b, bnk_m, bnk_v,
+    wv, bv, bnv_s, bnv_b, bnv_m, bnv_v,
+    out_q, out_k, out_v,
+):
+    nc = tc.nc
+    with ExitStack() as ctx:
+        consts = ctx.enter_context(tc.tile_pool(name="consts", bufs=1))
+        raws = ctx.enter_context(tc.tile_pool(name="raws", bufs=1))
+        stage = ctx.enter_context(tc.tile_pool(name="stage", bufs=3))
+        work = ctx.enter_context(tc.tile_pool(name="work", bufs=2))
+        rows = ctx.enter_context(tc.tile_pool(name="rows", bufs=4))
+        psum_kv = ctx.enter_context(tc.psum_pool(name="psum_kv", bufs=5))
+        psum_one = ctx.enter_context(tc.psum_pool(name="psum_one", bufs=1))
+        ctx.enter_context(tc.manual_schedule())
+
+        identity = consts.tile([P, P], F32)
+        make_identity(nc, identity[:])
+
+        w_rows = consts.tile([P, GROUPS, CHANNELS], BF16)
+        vector_rows = consts.tile([P, P], BF16)
+        nc.vector.memset(vector_rows[:], 0.0)
+
+        small_loads = [
+            (w_rows[:, 0, :], wq),
+            (w_rows[:, 1, :], wk),
+            (w_rows[:, 2:4, :], wv.rearrange("(g c) k -> c g k", g=2)),
+        ]
+        vectors_of_kind = (
+            (bq, bk, bv),
+            (bnq_s, bnk_s, bnv_s),
+            (bnq_b, bnk_b, bnv_b),
+            (bnq_m, bnk_m, bnv_m),
+            (bnq_v, bnk_v, bnv_v),
+        )
+        for kind in range(KINDS):
+            vec_q, vec_k, vec_v = vectors_of_kind[kind]
+            row = GROUPS * kind
+            small_loads.append((vector_rows[row : row + 1, :], vec_q.rearrange("(g c) -> g c", g=1)))
+            small_loads.append((vector_rows[row + 1 : row + 2, :], vec_k.rearrange("(g c) -> g c", g=1)))
+            small_loads.append((vector_rows[row + 2 : row + 4, :], vec_v.rearrange("(g c) -> g c", g=2)))
+
+        mem = memory.rearrange("b (p j) h w -> b p j (h w)", j=PACK)
+        raw_of_unit = []
+        for image in range(IMAGES):
+            load_width = UNIT if image == 0 else 2 * UNIT
+            for first in range(0, POSITIONS, load_width):
+                raw = raws.tile([P, PACK, load_width], BF16, name="raw_%d_%d" % (image, first))
+                nc.sync.dma_start(out=raw[:], in_=mem[image, :, :, first : first + load_width])
+                for start in range(0, load_width, UNIT):
+                    raw_of_unit.append(raw[:, :, start : start + UNIT])
+                for dst, src in small_loads[:SMALL_LOADS_PER_LARGE]:
+                    nc.sync.dma_start(out=dst, in_=src)
+                small_loads = small_loads[SMALL_LOADS_PER_LARGE:]
+
+        mem_codes = consts.tile([P, UNITS, UNIT], U32, align_bytes=64)
+        mem_scales = consts.tile([P, UNITS, UNIT], U8, align_bytes=64)
+        grouped_of = {}
+        sums_of = {}
+        peak_of = {}
+        z_q_of = {}
+        z_v_of = {}
+        t_q_of = {}
+        t_v_of = {}
+        k_of = {}
+
+        def regroup(unit):
+            grouped = stage.tile([P, UNIT, PACK], BF16, align_bytes=64)
+            dst = grouped[:].rearrange("p (c i) j -> p c j i", i=RUN)
+            src = raw_of_unit[unit].rearrange("p j (c i) -> p c j i", i=RUN)
+            nc.vector.tensor_copy(out=dst[:, :VECTOR_RUNS], in_=src[:, :VECTOR_RUNS])
+            nc.scalar.copy(out=dst[:, VECTOR_RUNS:], in_=src[:, VECTOR_RUNS:])
+            grouped_of[unit] = grouped
+
+        def quantise(unit):
+            nc.vector.quantize_mx(
+                out=mem_codes[:, unit, :].bitcast(FP8X4),
+                scales=mem_scales[:, unit, :],
+                in_=grouped_of[unit][:].rearrange("p n j -> p (n j)"),
+            )
+
+        def multiply(unit):
+            for group in range(GROUPS):
+                if group == GROUP_Q:
+                    acc = psum_one.tile([P, UNIT], F32, tag="acc_q")
+                else:
+                    acc = psum_kv.tile([P, UNIT], F32, tag="acc_kv")
+                nc.tensor.matmul_mx(
+                    out=acc[:],
+                    lhsT=w_codes[:, group * P : (group + 1) * P].bitcast(FP8X4),
+                    lhsT_scale=w_scales[:, group * P : (group + 1) * P],
+                    rhs=mem_codes[:, unit, :].bitcast(FP8X4),
+                    rhs_scale=mem_scales[:, unit, :],
+                    start=True,
+                    stop=True,
+                )
+                sums_of[(unit, group)] = acc
+
+        def normalise_q(unit):
+            z_q = work.tile([P, PACK, P], F32)
+            nc.scalar.activation(
+                out=z_q[:],
+                in_=sums_of[(unit, GROUP_Q)][:].rearrange("c (r i) -> c i r", i=PACK),
+                func=ACT.Identity,
+                scale=inv[:, GROUP_Q : GROUP_Q + 1],
+                bias=addend[:, GROUP_Q : GROUP_Q + 1],
+            )
+            z_q_of[unit] = z_q
+
+        def member(unit, group, a, b):
+            windows = sums_of[(unit, group)][:].rearrange(
+                "c (hh a ww b) -> c a b hh ww", a=2, ww=WIDTH // 2, b=2
+            )
+            return windows[:, a, b]
+
+        def peak_view(unit, group):
+            return peak_of[unit][:, group - 1, :].rearrange("c (hh ww) -> c hh ww", ww=WIDTH // 2)
+
+        def start_windows(unit, groups):
+            if unit not in peak_of:
+                peak = work.tile([P, len(POOLED_GROUPS), POOLED], F32)
+                peak_of[unit] = peak
+            for group in groups:
+                nc.scalar.activation(
+                    out=peak_view(unit, group),
+                    in_=member(unit, group, 0, 0),
+                    func=ACT.Copy,
+                    scale=inv[:, group : group + 1],
+                )
+
+        def fold_windows(unit):
+            for a, b in ((0, 1), (1, 0), (1, 1)):
+                for group in POOLED_GROUPS:
+                    nc.vector.scalar_tensor_tensor(
+                        out=peak_view(unit, group),
+                        in0=member(unit, group, a, b),
+                        scalar=inv[:, group : group + 1],
+                        in1=peak_view(unit, group),
+                        op0=ALU.mult,
+                        op1=ALU.max,
+                    )
+            image = unit // UNITS_PER_IMAGE
+            unit_in_image = unit % UNITS_PER_IMAGE
+            if unit_in_image == 0:
+                k_image = work.tile([P, UNITS_PER_IMAGE, POOLED], F32)
+                k_of[image] = k_image
+            z_v = work.tile([P, 2, POOLED], F32)
+            z_v_of[unit] = z_v
+            finished = (k_of[image][:, unit_in_image, :], z_v[:, 0, :], z_v[:, 1, :])
+            for group in POOLED_GROUPS:
+                nc.vector.tensor_scalar_add(
+                    out=finished[group - 1],
+                    in0=peak_of[unit][:, group - 1, :],
+                    scalar1=addend[:, group : group + 1],
+                )
+            if unit_in_image == UNITS_PER_IMAGE - 1:
+                nc.sync.dma_start(out=out_k[image], in_=k_of[image][:].rearrange("c u n -> c (u n)"))
+
+        def transpose_q(unit):
+            t_q = psum_one.tile([P, PACK, P], F32, tag="t_q")
+            for i in range(PACK):
+                nc.tensor.transpose(out=t_q[:, i, :], in_=z_q_of[unit][:, i, :], identity=identity[:])
+            t_q_of[unit] = t_q
+
+        def transpose_v(unit):
+            t_v = psum_one.tile([P, 2, P], F32, tag="t_v")
+            for half in range(2):
+                nc.tensor.transpose(out=t_v[:, half, :], in_=z_v_of[unit][:, half, :], identity=identity[:])
+            t_v_of[unit] = t_v
+
+        def store_q(unit):
+            q_rows = rows.tile([P, PACK, P], F32)
+            nc.scalar.copy(out=q_rows[:], in_=t_q_of[unit][:])
+            first = (unit % UNITS_PER_IMAGE) * UNIT
+            nc.sync.dma_start(
+                out=out_q[unit // UNITS_PER_IMAGE, first : first + UNIT, :].rearrange("(r i) c -> r i c", i=PACK),
+                in_=q_rows[:],
+            )
+
+        def store_v(unit):
+            v_rows = rows.tile([P, 2, P], F32)
+            nc.scalar.copy(out=v_rows[:], in_=t_v_of[unit][:])
+            first = (unit % UNITS_PER_IMAGE) * POOLED
+            nc.sync.dma_start(
+                out=out_v[unit // UNITS_PER_IMAGE, first : first + POOLED, :].rearrange("n (h c) -> n h c", h=2),
+                in_=v_rows[:],
+            )
+
+        regroup(0)
+
+        w_grouped = consts.tile([P, GROUPS * P * PACK], BF16, align_bytes=64)
+        w_grouped_words = w_grouped[:].bitcast(F32).rearrange("p (g c e) -> p g c e", g=GROUPS, e=2)
+        for half in range(2):
+            w_t = psum_kv.tile([P, 2, 2, P], F32, tag="acc_kv")
+            for g in range(2):
+                words = w_rows[:, 2 * half + g, :].bitcast(F32).rearrange("c (p e) -> c e p", e=2)
+                for e in range(2):
+                    nc.tensor.transpose(out=w_t[:, g, e, :], in_=words[:, e, :], identity=identity[:])
+            nc.vector.tensor_copy(
+                out=w_grouped_words[:, 2 * half : 2 * half + 2, :, :],
+                in_=w_t[:].rearrange("p g e c -> p g c e"),
+            )
+        w_codes = consts.tile([P, GROUPS * P], U32, align_bytes=64)
+        w_scales = consts.tile([P, GROUPS * P], U8, align_bytes=64)
+        nc.vector.quantize_mx(out=w_codes[:].bitcast(FP8X4), scales=w_scales[:], in_=w_grouped[:])
+
+        for unit in range(1, LEAD - 1):
+            regroup(unit)
+            quantise(unit - 1)
+
+        vector_rows_f32 = consts.tile([P, P], F32)
+        nc.vector.tensor_copy(out=vector_rows_f32[:], in_=vector_rows[:])
+        vector_t = psum_one.tile([P, P], F32, tag="t_v")
+        nc.tensor.transpose(out=vector_t[:], in_=vector_rows_f32[:], identity=identity[:])
+        per_channel = consts.tile([P, KINDS, GROUPS], F32)
+        nc.vector.tensor_copy(
+            out=per_channel[:],
+            in_=vector_t[:, 0 : KINDS * GROUPS].rearrange("p (k g) -> p k g", g=GROUPS),
+        )
+        variance_eps = consts.tile([P, GROUPS], F32)
+        nc.vector.tensor_scalar_add(out=variance_eps[:], in0=per_channel[:, VARIANCE, :], scalar1=EPS)
+        deviation = consts.tile([P, GROUPS], F32)
+        nc.scalar.sqrt(out=deviation[:], in_=variance_eps[:])
+        inv_deviation = consts.tile([P, GROUPS], F32)
+        nc.vector.reciprocal(out=inv_deviation[:], in_=deviation[:])
+        inv = consts.tile([P, GROUPS], F32)
+        nc.vector.tensor_mul(out=inv[:], in0=per_channel[:, GAIN, :], in1=inv_deviation[:])
+        centred = consts.tile([P, GROUPS], F32)
+        nc.vector.tensor_sub(out=centred[:], in0=per_channel[:, BIAS, :], in1=per_channel[:, MEAN, :])
+        centred_scaled = consts.tile([P, GROUPS], F32)
+        nc.vector.tensor_mul(out=centred_scaled[:], in0=centred[:], in1=inv[:])
+        addend = consts.tile([P, GROUPS], F32)
+        nc.vector.tensor_add(out=addend[:], in0=centred_scaled[:], in1=per_channel[:, SHIFT, :])
+
+        def live(unit):
+            return 0 <= unit < UNITS
+
+        for step in range(-1, UNITS + 1):
+            if live(step + 1):
+                multiply(step + 1)
+            if live(step):
+                store_q(step)
+            if live(step - 1):
+                store_v(step - 1)
+            if live(step + 1):
+                start_windows(step + 1, POOLED_GROUPS[:2])
+                normalise_q(step + 1)
+            if live(step):
+                fold_windows(step)
+            if live(step + 1):
+                transpose_q(step + 1)
+            if live(step):
+                transpose_v(step)
+            if live(step + LEAD):
+                regroup(step + LEAD)
+            if live(step + 1):
+                start_windows(step + 1, POOLED_GROUPS[2:])
+            if live(step + LEAD - 1):
+                quantise(step + LEAD - 1)

@@ -37,8 +37,8 @@ SHIFT = 2
 MEAN = 3
 VARIANCE = 4
 
-VECTOR_RUNS = 80
-LEAD = 5
+VECTOR_RUNS = 64
+LEAD = 8
 
 SMALL_LOADS_PER_LARGE = 3
 
@@ -285,25 +285,25 @@ def tile_selfattention_pa_t_kernel(
         def live(unit):
             return 0 <= unit < UNITS
 
-        for step in range(-1, UNITS + 1):
+        for step in range(-1, UNITS + 2):
             if live(step + 1):
                 multiply(step + 1)
             if live(step):
-                store_q(step)
+                transpose_q(step)
             if live(step - 1):
-                store_v(step - 1)
+                transpose_v(step - 1)
             if live(step + 1):
                 start_windows(step + 1, POOLED_GROUPS[:2])
                 normalise_q(step + 1)
             if live(step):
                 fold_windows(step)
-            if live(step + 1):
-                transpose_q(step + 1)
-            if live(step):
-                transpose_v(step)
             if live(step + LEAD):
                 regroup(step + LEAD)
             if live(step + 1):
                 start_windows(step + 1, POOLED_GROUPS[2:])
+            if live(step):
+                store_q(step)
+            if live(step - 1):
+                store_v(step - 1)
             if live(step + LEAD - 1):
                 quantise(step + LEAD - 1)

@@ -37,7 +37,8 @@ SHIFT = 2
 MEAN = 3
 VARIANCE = 4
 
-VECTOR_RUNS = 64
+HEAD_SPLIT = (64, 128)
+STEP_SPLIT = (48, 96)
 LEAD = 8
 
 SMALL_LOADS_PER_LARGE = 3
@@ -114,12 +115,22 @@ def tile_selfattention_pa_t_kernel(
         t_v_of = {}
         k_of = {}
 
-        def regroup(unit):
+        def regroup(unit, split):
             grouped = stage.tile([P, UNIT, PACK], BF16, align_bytes=64)
             dst = grouped[:].rearrange("p (c i) j -> p c j i", i=RUN)
             src = raw_of_unit[unit].rearrange("p j (c i) -> p c j i", i=RUN)
-            nc.vector.tensor_copy(out=dst[:, :VECTOR_RUNS], in_=src[:, :VECTOR_RUNS])
-            nc.scalar.copy(out=dst[:, VECTOR_RUNS:], in_=src[:, VECTOR_RUNS:])
+            vector_end, scalar_end = split
+            nc.vector.tensor_copy(out=dst[:, :vector_end], in_=src[:, :vector_end])
+            nc.scalar.copy(out=dst[:, vector_end:scalar_end], in_=src[:, vector_end:scalar_end])
+            if scalar_end < UNIT // RUN:
+                nc.gpsimd.tensor_scalar(
+                    out=dst[:, scalar_end:],
+                    in0=src[:, scalar_end:],
+                    scalar1=1.0,
+                    scalar2=0.0,
+                    op0=ALU.mult,
+                    op1=ALU.add,
+                )
             grouped_of[unit] = grouped
 
         def quantise(unit):
@@ -236,7 +247,7 @@ def tile_selfattention_pa_t_kernel(
                 in_=v_rows[:],
             )
 
-        regroup(0)
+        regroup(0, HEAD_SPLIT)
 
         w_grouped = consts.tile([P, GROUPS * P * PACK], BF16, align_bytes=64)
         w_grouped_words = w_grouped[:].bitcast(F32).rearrange("p (g c e) -> p g c e", g=GROUPS, e=2)
@@ -255,7 +266,7 @@ def tile_selfattention_pa_t_kernel(
         nc.vector.quantize_mx(out=w_codes[:].bitcast(FP8X4), scales=w_scales[:], in_=w_grouped[:])
 
         for unit in range(1, LEAD - 1):
-            regroup(unit)
+            regroup(unit, HEAD_SPLIT)
             quantise(unit - 1)
 
         vector_rows_f32 = consts.tile([P, P], F32)
@@ -298,7 +309,7 @@ def tile_selfattention_pa_t_kernel(
             if live(step):
                 fold_windows(step)
             if live(step + LEAD):
-                regroup(step + LEAD)
+                regroup(step + LEAD, STEP_SPLIT)
             if live(step + 1):
                 start_windows(step + 1, POOLED_GROUPS[2:])
             if live(step):

@@ -38,10 +38,14 @@ MEAN = 3
 VARIANCE = 4
 
 HEAD_SPLIT = (64, 128)
-STEP_SPLIT = (48, 96)
-LEAD = 8
+STEP_SPLIT = (40, 80)
+FIRST_SHARED = 2
+VECTOR = 0
+SCALAR = 1
+GPSIMD = 2
+LEAD = 3
 
-SMALL_LOADS_PER_LARGE = 3
+SMALL_LOADS_PER_LARGE = 5
 
 FLOPS = 2 * IMAGES * POSITIONS * CHANNELS * GROUPS * P
 
@@ -58,7 +62,6 @@ def tile_selfattention_pa_t_kernel(
     with ExitStack() as ctx:
         consts = ctx.enter_context(tc.tile_pool(name="consts", bufs=1))
         raws = ctx.enter_context(tc.tile_pool(name="raws", bufs=1))
-        stage = ctx.enter_context(tc.tile_pool(name="stage", bufs=3))
         work = ctx.enter_context(tc.tile_pool(name="work", bufs=2))
         rows = ctx.enter_context(tc.tile_pool(name="rows", bufs=4))
         psum_kv = ctx.enter_context(tc.psum_pool(name="psum_kv", bufs=5))
@@ -72,11 +75,12 @@ def tile_selfattention_pa_t_kernel(
         vector_rows = consts.tile([P, P], BF16)
         nc.vector.memset(vector_rows[:], 0.0)
 
-        small_loads = [
+        weight_loads = [
             (w_rows[:, 0, :], wq),
             (w_rows[:, 1, :], wk),
             (w_rows[:, 2:4, :], wv.rearrange("(g c) k -> c g k", g=2)),
         ]
+        small_loads = []
         vectors_of_kind = (
             (bq, bk, bv),
             (bnq_s, bnk_s, bnv_s),
@@ -100,13 +104,17 @@ def tile_selfattention_pa_t_kernel(
                 nc.sync.dma_start(out=raw[:], in_=mem[image, :, :, first : first + load_width])
                 for start in range(0, load_width, UNIT):
                     raw_of_unit.append(raw[:, :, start : start + UNIT])
-                for dst, src in small_loads[:SMALL_LOADS_PER_LARGE]:
+                for dst, src in weight_loads:
                     nc.sync.dma_start(out=dst, in_=src)
-                small_loads = small_loads[SMALL_LOADS_PER_LARGE:]
+                if not weight_loads:
+                    for dst, src in small_loads[:SMALL_LOADS_PER_LARGE]:
+                        nc.sync.dma_start(out=dst, in_=src)
+                    small_loads = small_loads[SMALL_LOADS_PER_LARGE:]
+                weight_loads = []
 
         mem_codes = consts.tile([P, UNITS, UNIT], U32, align_bytes=64)
         mem_scales = consts.tile([P, UNITS, UNIT], U8, align_bytes=64)
-        grouped_of = {}
+        grouped = consts.tile([P, UNITS, UNIT, PACK], BF16, align_bytes=64)
         sums_of = {}
         peak_of = {}
         z_q_of = {}
@@ -115,14 +123,19 @@ def tile_selfattention_pa_t_kernel(
         t_v_of = {}
         k_of = {}
 
-        def regroup(unit, split):
-            grouped = stage.tile([P, UNIT, PACK], BF16, align_bytes=64)
-            dst = grouped[:].rearrange("p (c i) j -> p c j i", i=RUN)
+        def split_of(unit):
+            return HEAD_SPLIT if unit < FIRST_SHARED else STEP_SPLIT
+
+        def regroup(unit, engines):
+            split = split_of(unit)
+            dst = grouped[:, unit].rearrange("p (c i) j -> p c j i", i=RUN)
             src = raw_of_unit[unit].rearrange("p j (c i) -> p c j i", i=RUN)
             vector_end, scalar_end = split
-            nc.vector.tensor_copy(out=dst[:, :vector_end], in_=src[:, :vector_end])
-            nc.scalar.copy(out=dst[:, vector_end:scalar_end], in_=src[:, vector_end:scalar_end])
-            if scalar_end < UNIT // RUN:
+            if VECTOR in engines:
+                nc.vector.tensor_copy(out=dst[:, :vector_end], in_=src[:, :vector_end])
+            if SCALAR in engines:
+                nc.scalar.copy(out=dst[:, vector_end:scalar_end], in_=src[:, vector_end:scalar_end])
+            if GPSIMD in engines and scalar_end < UNIT // RUN:
                 nc.gpsimd.tensor_scalar(
                     out=dst[:, scalar_end:],
                     in0=src[:, scalar_end:],
@@ -131,13 +144,12 @@ def tile_selfattention_pa_t_kernel(
                     op0=ALU.mult,
                     op1=ALU.add,
                 )
-            grouped_of[unit] = grouped
 
         def quantise(unit):
             nc.vector.quantize_mx(
                 out=mem_codes[:, unit, :].bitcast(FP8X4),
                 scales=mem_scales[:, unit, :],
-                in_=grouped_of[unit][:].rearrange("p n j -> p (n j)"),
+                in_=grouped[:, unit].rearrange("p n j -> p (n j)"),
             )
 
         def multiply(unit):
@@ -190,16 +202,6 @@ def tile_selfattention_pa_t_kernel(
                 )
 
         def fold_windows(unit):
-            for a, b in ((0, 1), (1, 0), (1, 1)):
-                for group in POOLED_GROUPS:
-                    nc.vector.scalar_tensor_tensor(
-                        out=peak_view(unit, group),
-                        in0=member(unit, group, a, b),
-                        scalar=inv[:, group : group + 1],
-                        in1=peak_view(unit, group),
-                        op0=ALU.mult,
-                        op1=ALU.max,
-                    )
             image = unit // UNITS_PER_IMAGE
             unit_in_image = unit % UNITS_PER_IMAGE
             if unit_in_image == 0:
@@ -208,14 +210,28 @@ def tile_selfattention_pa_t_kernel(
             z_v = work.tile([P, 2, POOLED], F32)
             z_v_of[unit] = z_v
             finished = (k_of[image][:, unit_in_image, :], z_v[:, 0, :], z_v[:, 1, :])
-            for group in POOLED_GROUPS:
-                nc.vector.tensor_scalar_add(
-                    out=finished[group - 1],
-                    in0=peak_of[unit][:, group - 1, :],
-                    scalar1=addend[:, group : group + 1],
-                )
+            for a, b in ((0, 1), (1, 0), (1, 1)):
+                for group in POOLED_GROUPS:
+                    if (a, b) == (1, 1):
+                        target = finished[group - 1].rearrange("c (hh ww) -> c hh ww", ww=WIDTH // 2)
+                    else:
+                        target = peak_view(unit, group)
+                    nc.vector.scalar_tensor_tensor(
+                        out=target,
+                        in0=member(unit, group, a, b),
+                        scalar=inv[:, group : group + 1],
+                        in1=peak_view(unit, group),
+                        op0=ALU.mult,
+                        op1=ALU.max,
+                    )
             if unit_in_image == UNITS_PER_IMAGE - 1:
-                nc.sync.dma_start(out=out_k[image], in_=k_of[image][:].rearrange("c u n -> c (u n)"))
+                k_rows = work.tile([P, UNITS_PER_IMAGE * POOLED], F32)
+                nc.vector.tensor_scalar_add(
+                    out=k_rows[:],
+                    in0=k_of[image][:].rearrange("c u n -> c (u n)"),
+                    scalar1=addend[:, GROUP_K : GROUP_K + 1],
+                )
+                nc.sync.dma_start(out=out_k[image], in_=k_rows[:])
 
         def transpose_q(unit):
             t_q = psum_one.tile([P, PACK, P], F32, tag="t_q")
@@ -226,7 +242,23 @@ def tile_selfattention_pa_t_kernel(
         def transpose_v(unit):
             t_v = psum_one.tile([P, 2, P], F32, tag="t_v")
             for half in range(2):
-                nc.tensor.transpose(out=t_v[:, half, :], in_=z_v_of[unit][:, half, :], identity=identity[:])
+                group = POOLED_GROUPS[1 + half]
+                nc.tensor.matmul(
+                    out=t_v[:, half, :],
+                    lhsT=addend[:, group : group + 1].to_broadcast([P, P]),
+                    rhs=identity[:],
+                    is_transpose=True,
+                    start=True,
+                    stop=False,
+                )
+                nc.tensor.matmul(
+                    out=t_v[:, half, :],
+                    lhsT=z_v_of[unit][:, half, :],
+                    rhs=identity[:],
+                    is_transpose=True,
+                    start=False,
+                    stop=True,
+                )
             t_v_of[unit] = t_v
 
         def store_q(unit):
@@ -247,7 +279,14 @@ def tile_selfattention_pa_t_kernel(
                 in_=v_rows[:],
             )
 
-        regroup(0, HEAD_SPLIT)
+        warm = consts.tile([P, 2], F32)
+        nc.vector.memset(warm[:], 1.0)
+        nc.scalar.sqrt(out=warm[:, 1:2], in_=warm[:, 0:1])
+
+        for unit in range(FIRST_SHARED, UNITS):
+            regroup(unit, (GPSIMD,))
+
+        regroup(0, (VECTOR, SCALAR))
 
         w_grouped = consts.tile([P, GROUPS * P * PACK], BF16, align_bytes=64)
         w_grouped_words = w_grouped[:].bitcast(F32).rearrange("p (g c e) -> p g c e", g=GROUPS, e=2)
@@ -265,14 +304,14 @@ def tile_selfattention_pa_t_kernel(
         w_scales = consts.tile([P, GROUPS * P], U8, align_bytes=64)
         nc.vector.quantize_mx(out=w_codes[:].bitcast(FP8X4), scales=w_scales[:], in_=w_grouped[:])
 
-        for unit in range(1, LEAD - 1):
-            regroup(unit, HEAD_SPLIT)
-            quantise(unit - 1)
+        regroup(1, (VECTOR, SCALAR))
+        quantise(0)
 
         vector_rows_f32 = consts.tile([P, P], F32)
         nc.vector.tensor_copy(out=vector_rows_f32[:], in_=vector_rows[:])
         vector_t = psum_one.tile([P, P], F32, tag="t_v")
         nc.tensor.transpose(out=vector_t[:], in_=vector_rows_f32[:], identity=identity[:])
+        regroup(2, (VECTOR, SCALAR))
         per_channel = consts.tile([P, KINDS, GROUPS], F32)
         nc.vector.tensor_copy(
             out=per_channel[:],
@@ -282,12 +321,13 @@ def tile_selfattention_pa_t_kernel(
         nc.vector.tensor_scalar_add(out=variance_eps[:], in0=per_channel[:, VARIANCE, :], scalar1=EPS)
         deviation = consts.tile([P, GROUPS], F32)
         nc.scalar.sqrt(out=deviation[:], in_=variance_eps[:])
+        centred = consts.tile([P, GROUPS], F32)
+        nc.vector.tensor_sub(out=centred[:], in0=per_channel[:, BIAS, :], in1=per_channel[:, MEAN, :])
+        quantise(1)
         inv_deviation = consts.tile([P, GROUPS], F32)
         nc.vector.reciprocal(out=inv_deviation[:], in_=deviation[:])
         inv = consts.tile([P, GROUPS], F32)
         nc.vector.tensor_mul(out=inv[:], in0=per_channel[:, GAIN, :], in1=inv_deviation[:])
-        centred = consts.tile([P, GROUPS], F32)
-        nc.vector.tensor_sub(out=centred[:], in0=per_channel[:, BIAS, :], in1=per_channel[:, MEAN, :])
         centred_scaled = consts.tile([P, GROUPS], F32)
         nc.vector.tensor_mul(out=centred_scaled[:], in0=centred[:], in1=inv[:])
         addend = consts.tile([P, GROUPS], F32)
@@ -308,13 +348,13 @@ def tile_selfattention_pa_t_kernel(
                 normalise_q(step + 1)
             if live(step):
                 fold_windows(step)
-            if live(step + LEAD):
-                regroup(step + LEAD, STEP_SPLIT)
+            if step >= 0 and live(step + LEAD):
+                regroup(step + LEAD, (VECTOR, SCALAR))
             if live(step + 1):
                 start_windows(step + 1, POOLED_GROUPS[2:])
             if live(step):
                 store_q(step)
             if live(step - 1):
                 store_v(step - 1)
-            if live(step + LEAD - 1):
+            if step >= 0 and live(step + LEAD - 1):
                 quantise(step + LEAD - 1)

@@ -39,10 +39,7 @@ VARIANCE = 4
 
 HEAD_SPLIT = (64, 128)
 STEP_SPLIT = (40, 80)
-FIRST_SHARED = 2
-VECTOR = 0
-SCALAR = 1
-GPSIMD = 2
+FIRST_SHARED = 3
 LEAD = 3
 
 SMALL_LOADS_PER_LARGE = 5
@@ -62,6 +59,7 @@ def tile_selfattention_pa_t_kernel(
     with ExitStack() as ctx:
         consts = ctx.enter_context(tc.tile_pool(name="consts", bufs=1))
         raws = ctx.enter_context(tc.tile_pool(name="raws", bufs=1))
+        stage = ctx.enter_context(tc.tile_pool(name="stage", bufs=2))
         work = ctx.enter_context(tc.tile_pool(name="work", bufs=2))
         rows = ctx.enter_context(tc.tile_pool(name="rows", bufs=4))
         psum_kv = ctx.enter_context(tc.psum_pool(name="psum_kv", bufs=5))
@@ -114,7 +112,7 @@ def tile_selfattention_pa_t_kernel(
 
         mem_codes = consts.tile([P, UNITS, UNIT], U32, align_bytes=64)
         mem_scales = consts.tile([P, UNITS, UNIT], U8, align_bytes=64)
-        grouped = consts.tile([P, UNITS, UNIT, PACK], BF16, align_bytes=64)
+        grouped_of = {}
         sums_of = {}
         peak_of = {}
         z_q_of = {}
@@ -126,16 +124,16 @@ def tile_selfattention_pa_t_kernel(
         def split_of(unit):
             return HEAD_SPLIT if unit < FIRST_SHARED else STEP_SPLIT
 
-        def regroup(unit, engines):
+        def regroup(unit):
             split = split_of(unit)
-            dst = grouped[:, unit].rearrange("p (c i) j -> p c j i", i=RUN)
+            grouped = stage.tile([P, UNIT, PACK], BF16, align_bytes=64)
+            grouped_of[unit] = grouped
+            dst = grouped[:].rearrange("p (c i) j -> p c j i", i=RUN)
             src = raw_of_unit[unit].rearrange("p j (c i) -> p c j i", i=RUN)
             vector_end, scalar_end = split
-            if VECTOR in engines:
-                nc.vector.tensor_copy(out=dst[:, :vector_end], in_=src[:, :vector_end])
-            if SCALAR in engines:
-                nc.scalar.copy(out=dst[:, vector_end:scalar_end], in_=src[:, vector_end:scalar_end])
-            if GPSIMD in engines and scalar_end < UNIT // RUN:
+            nc.vector.tensor_copy(out=dst[:, :vector_end], in_=src[:, :vector_end])
+            nc.scalar.copy(out=dst[:, vector_end:scalar_end], in_=src[:, vector_end:scalar_end])
+            if scalar_end < UNIT // RUN:
                 nc.gpsimd.tensor_scalar(
                     out=dst[:, scalar_end:],
                     in0=src[:, scalar_end:],
@@ -149,7 +147,7 @@ def tile_selfattention_pa_t_kernel(
             nc.vector.quantize_mx(
                 out=mem_codes[:, unit, :].bitcast(FP8X4),
                 scales=mem_scales[:, unit, :],
-                in_=grouped[:, unit].rearrange("p n j -> p (n j)"),
+                in_=grouped_of[unit][:].rearrange("p n j -> p (n j)"),
             )
 
         def multiply(unit):
@@ -283,10 +281,7 @@ def tile_selfattention_pa_t_kernel(
         nc.vector.memset(warm[:], 1.0)
         nc.scalar.sqrt(out=warm[:, 1:2], in_=warm[:, 0:1])
 
-        for unit in range(FIRST_SHARED, UNITS):
-            regroup(unit, (GPSIMD,))
-
-        regroup(0, (VECTOR, SCALAR))
+        regroup(0)
 
         w_grouped = consts.tile([P, GROUPS * P * PACK], BF16, align_bytes=64)
         w_grouped_words = w_grouped[:].bitcast(F32).rearrange("p (g c e) -> p g c e", g=GROUPS, e=2)
@@ -304,14 +299,14 @@ def tile_selfattention_pa_t_kernel(
         w_scales = consts.tile([P, GROUPS * P], U8, align_bytes=64)
         nc.vector.quantize_mx(out=w_codes[:].bitcast(FP8X4), scales=w_scales[:], in_=w_grouped[:])
 
-        regroup(1, (VECTOR, SCALAR))
+        regroup(1)
         quantise(0)
 
         vector_rows_f32 = consts.tile([P, P], F32)
         nc.vector.tensor_copy(out=vector_rows_f32[:], in_=vector_rows[:])
         vector_t = psum_one.tile([P, P], F32, tag="t_v")
         nc.tensor.transpose(out=vector_t[:], in_=vector_rows_f32[:], identity=identity[:])
-        regroup(2, (VECTOR, SCALAR))
+        regroup(2)
         per_channel = consts.tile([P, KINDS, GROUPS], F32)
         nc.vector.tensor_copy(
             out=per_channel[:],
@@ -323,7 +318,6 @@ def tile_selfattention_pa_t_kernel(
         nc.scalar.sqrt(out=deviation[:], in_=variance_eps[:])
         centred = consts.tile([P, GROUPS], F32)
         nc.vector.tensor_sub(out=centred[:], in0=per_channel[:, BIAS, :], in1=per_channel[:, MEAN, :])
-        quantise(1)
         inv_deviation = consts.tile([P, GROUPS], F32)
         nc.vector.reciprocal(out=inv_deviation[:], in_=deviation[:])
         inv = consts.tile([P, GROUPS], F32)
@@ -332,6 +326,7 @@ def tile_selfattention_pa_t_kernel(
         nc.vector.tensor_mul(out=centred_scaled[:], in0=centred[:], in1=inv[:])
         addend = consts.tile([P, GROUPS], F32)
         nc.vector.tensor_add(out=addend[:], in0=centred_scaled[:], in1=per_channel[:, SHIFT, :])
+        quantise(1)
 
         def live(unit):
             return 0 <= unit < UNITS
@@ -349,7 +344,7 @@ def tile_selfattention_pa_t_kernel(
             if live(step):
                 fold_windows(step)
             if step >= 0 and live(step + LEAD):
-                regroup(step + LEAD, (VECTOR, SCALAR))
+                regroup(step + LEAD)
             if live(step + 1):
                 start_windows(step + 1, POOLED_GROUPS[2:])
             if live(step):

@@ -38,7 +38,7 @@ MEAN = 3
 VARIANCE = 4
 
 HEAD_SPLIT = (64, 128)
-STEP_SPLIT = (40, 80)
+STEP_SPLIT = (48, 80)
 FIRST_SHARED = 3
 LEAD = 3
 
@@ -341,12 +341,12 @@ def tile_selfattention_pa_t_kernel(
             if live(step + 1):
                 start_windows(step + 1, POOLED_GROUPS[:2])
                 normalise_q(step + 1)
+            if live(step + 1):
+                start_windows(step + 1, POOLED_GROUPS[2:])
             if live(step):
                 fold_windows(step)
             if step >= 0 and live(step + LEAD):
                 regroup(step + LEAD)
-            if live(step + 1):
-                start_windows(step + 1, POOLED_GROUPS[2:])
             if live(step):
                 store_q(step)
             if live(step - 1):

@@ -42,8 +42,6 @@ STEP_SPLIT = (48, 80)
 FIRST_SHARED = 3
 LEAD = 3
 
-SMALL_LOADS_PER_LARGE = 5
-
 FLOPS = 2 * IMAGES * POSITIONS * CHANNELS * GROUPS * P
 
 
@@ -68,6 +66,8 @@ def tile_selfattention_pa_t_kernel(
 
         identity = consts.tile([P, P], F32)
         make_identity(nc, identity[:])
+        identity_bf16 = consts.tile([P, P], BF16)
+        make_identity(nc, identity_bf16[:])
 
         w_rows = consts.tile([P, GROUPS, CHANNELS], BF16)
         vector_rows = consts.tile([P, P], BF16)
@@ -95,6 +95,7 @@ def tile_selfattention_pa_t_kernel(
 
         mem = memory.rearrange("b (p j) h w -> b p j (h w)", j=PACK)
         raw_of_unit = []
+        vectors_behind = (4, 6, 5)
         for image in range(IMAGES):
             load_width = UNIT if image == 0 else 2 * UNIT
             for first in range(0, POSITIONS, load_width):
@@ -104,11 +105,11 @@ def tile_selfattention_pa_t_kernel(
                     raw_of_unit.append(raw[:, :, start : start + UNIT])
                 for dst, src in weight_loads:
                     nc.sync.dma_start(out=dst, in_=src)
-                if not weight_loads:
-                    for dst, src in small_loads[:SMALL_LOADS_PER_LARGE]:
-                        nc.sync.dma_start(out=dst, in_=src)
-                    small_loads = small_loads[SMALL_LOADS_PER_LARGE:]
                 weight_loads = []
+                for dst, src in small_loads[: vectors_behind[0]]:
+                    nc.sync.dma_start(out=dst, in_=src)
+                small_loads = small_loads[vectors_behind[0] :]
+                vectors_behind = vectors_behind[1:] + (0,)
 
         mem_codes = consts.tile([P, UNITS, UNIT], U32, align_bytes=64)
         mem_scales = consts.tile([P, UNITS, UNIT], U8, align_bytes=64)
@@ -150,8 +151,8 @@ def tile_selfattention_pa_t_kernel(
                 in_=grouped_of[unit][:].rearrange("p n j -> p (n j)"),
             )
 
-        def multiply(unit):
-            for group in range(GROUPS):
+        def multiply(unit, groups):
+            for group in groups:
                 if group == GROUP_Q:
                     acc = psum_one.tile([P, UNIT], F32, tag="acc_q")
                 else:
@@ -291,49 +292,51 @@ def tile_selfattention_pa_t_kernel(
                 words = w_rows[:, 2 * half + g, :].bitcast(F32).rearrange("c (p e) -> c e p", e=2)
                 for e in range(2):
                     nc.tensor.transpose(out=w_t[:, g, e, :], in_=words[:, e, :], identity=identity[:])
-            nc.vector.tensor_copy(
-                out=w_grouped_words[:, 2 * half : 2 * half + 2, :, :],
-                in_=w_t[:].rearrange("p g e c -> p g c e"),
-            )
+            if half == 0:
+                nc.vector.tensor_copy(
+                    out=w_grouped_words[:, 0:2, :, :], in_=w_t[:].rearrange("p g e c -> p g c e")
+                )
+            else:
+                nc.scalar.copy(out=w_grouped_words[:, 2:4, :, :], in_=w_t[:].rearrange("p g e c -> p g c e"))
+        quantise(0)
         w_codes = consts.tile([P, GROUPS * P], U32, align_bytes=64)
         w_scales = consts.tile([P, GROUPS * P], U8, align_bytes=64)
         nc.vector.quantize_mx(out=w_codes[:].bitcast(FP8X4), scales=w_scales[:], in_=w_grouped[:])
-
+        multiply(0, (GROUP_Q,))
         regroup(1)
-        quantise(0)
 
-        vector_rows_f32 = consts.tile([P, P], F32)
-        nc.vector.tensor_copy(out=vector_rows_f32[:], in_=vector_rows[:])
-        vector_t = psum_one.tile([P, P], F32, tag="t_v")
-        nc.tensor.transpose(out=vector_t[:], in_=vector_rows_f32[:], identity=identity[:])
-        regroup(2)
+        vector_t = psum_one.tile([P, P], BF16, tag="t_v")
+        nc.tensor.transpose(out=vector_t[:], in_=vector_rows[:], identity=identity_bf16[:])
+        multiply(0, POOLED_GROUPS)
+        deviation = consts.tile([P, GROUPS], F32)
+        nc.scalar.activation(
+            out=deviation[:],
+            in_=vector_t[:, VARIANCE * GROUPS : (VARIANCE + 1) * GROUPS],
+            func=ACT.Sqrt,
+            bias=EPS,
+        )
         per_channel = consts.tile([P, KINDS, GROUPS], F32)
         nc.vector.tensor_copy(
             out=per_channel[:],
             in_=vector_t[:, 0 : KINDS * GROUPS].rearrange("p (k g) -> p k g", g=GROUPS),
         )
-        variance_eps = consts.tile([P, GROUPS], F32)
-        nc.vector.tensor_scalar_add(out=variance_eps[:], in0=per_channel[:, VARIANCE, :], scalar1=EPS)
-        deviation = consts.tile([P, GROUPS], F32)
-        nc.scalar.sqrt(out=deviation[:], in_=variance_eps[:])
-        centred = consts.tile([P, GROUPS], F32)
-        nc.vector.tensor_sub(out=centred[:], in0=per_channel[:, BIAS, :], in1=per_channel[:, MEAN, :])
         inv_deviation = consts.tile([P, GROUPS], F32)
         nc.vector.reciprocal(out=inv_deviation[:], in_=deviation[:])
         inv = consts.tile([P, GROUPS], F32)
         nc.vector.tensor_mul(out=inv[:], in0=per_channel[:, GAIN, :], in1=inv_deviation[:])
+        centred = consts.tile([P, GROUPS], F32)
+        nc.vector.tensor_sub(out=centred[:], in0=per_channel[:, BIAS, :], in1=per_channel[:, MEAN, :])
         centred_scaled = consts.tile([P, GROUPS], F32)
         nc.vector.tensor_mul(out=centred_scaled[:], in0=centred[:], in1=inv[:])
         addend = consts.tile([P, GROUPS], F32)
         nc.vector.tensor_add(out=addend[:], in0=centred_scaled[:], in1=per_channel[:, SHIFT, :])
-        quantise(1)
 
         def live(unit):
             return 0 <= unit < UNITS
 
         for step in range(-1, UNITS + 2):
-            if live(step + 1):
-                multiply(step + 1)
+            if step >= 0 and live(step + 1):
+                multiply(step + 1, range(GROUPS))
             if live(step):
                 transpose_q(step)
             if live(step - 1):
@@ -345,11 +348,11 @@ def tile_selfattention_pa_t_kernel(
                 start_windows(step + 1, POOLED_GROUPS[2:])
             if live(step):
                 fold_windows(step)
-            if step >= 0 and live(step + LEAD):
+            if live(step + LEAD):
                 regroup(step + LEAD)
             if live(step):
                 store_q(step)
             if live(step - 1):
                 store_v(step - 1)
-            if step >= 0 and live(step + LEAD - 1):
+            if live(step + LEAD - 1):
                 quantise(step + LEAD - 1)

@@ -136,8 +136,8 @@ def tile_selfattention_pa_t_kernel(
             nc.scalar.copy(out=dst[:, vector_end:scalar_end], in_=src[:, vector_end:scalar_end])
             if scalar_end < UNIT // RUN:
                 nc.gpsimd.tensor_scalar(
-                    out=dst[:, scalar_end:],
-                    in0=src[:, scalar_end:],
+                    out=grouped[:, scalar_end * RUN :, :],
+                    in0=raw_of_unit[unit][:, :, scalar_end * RUN :].rearrange("p j n -> p n j"),
                     scalar1=1.0,
                     scalar2=0.0,
                     op0=ALU.mult,

@@ -38,8 +38,10 @@ MEAN = 3
 VARIANCE = 4
 
 HEAD_SPLIT = (64, 128)
-STEP_SPLIT = (48, 80)
+STEP_SPLIT = (40, 64)
 FIRST_SHARED = 3
+VECTOR_AND_SCALAR = 0
+GPSIMD = 1
 LEAD = 3
 
 FLOPS = 2 * IMAGES * POSITIONS * CHANNELS * GROUPS * P
@@ -125,16 +127,19 @@ def tile_selfattention_pa_t_kernel(
         def split_of(unit):
             return HEAD_SPLIT if unit < FIRST_SHARED else STEP_SPLIT
 
-        def regroup(unit):
+        def regroup(unit, engines):
             split = split_of(unit)
-            grouped = stage.tile([P, UNIT, PACK], BF16, align_bytes=64)
-            grouped_of[unit] = grouped
+            if unit not in grouped_of:
+                new_tile = stage.tile([P, UNIT, PACK], BF16, align_bytes=64, tag="grouped")
+                grouped_of[unit] = new_tile
+            grouped = grouped_of[unit]
             dst = grouped[:].rearrange("p (c i) j -> p c j i", i=RUN)
             src = raw_of_unit[unit].rearrange("p j (c i) -> p c j i", i=RUN)
             vector_end, scalar_end = split
-            nc.vector.tensor_copy(out=dst[:, :vector_end], in_=src[:, :vector_end])
-            nc.scalar.copy(out=dst[:, vector_end:scalar_end], in_=src[:, vector_end:scalar_end])
-            if scalar_end < UNIT // RUN:
+            if VECTOR_AND_SCALAR in engines:
+                nc.vector.tensor_copy(out=dst[:, :vector_end], in_=src[:, :vector_end])
+                nc.scalar.copy(out=dst[:, vector_end:scalar_end], in_=src[:, vector_end:scalar_end])
+            if GPSIMD in engines and scalar_end < UNIT // RUN:
                 nc.gpsimd.tensor_scalar(
                     out=grouped[:, scalar_end * RUN :, :],
                     in0=raw_of_unit[unit][:, :, scalar_end * RUN :].rearrange("p j n -> p n j"),
@@ -271,7 +276,10 @@ def tile_selfattention_pa_t_kernel(
 
         def store_v(unit):
             v_rows = rows.tile([P, 2, P], F32)
-            nc.scalar.copy(out=v_rows[:], in_=t_v_of[unit][:])
+            if unit < UNITS - 2:
+                nc.scalar.copy(out=v_rows[:], in_=t_v_of[unit][:])
+            else:
+                nc.vector.tensor_copy(out=v_rows[:], in_=t_v_of[unit][:])
             first = (unit % UNITS_PER_IMAGE) * POOLED
             nc.sync.dma_start(
                 out=out_v[unit // UNITS_PER_IMAGE, first : first + POOLED, :].rearrange("n (h c) -> n h c", h=2),
@@ -282,7 +290,7 @@ def tile_selfattention_pa_t_kernel(
         nc.vector.memset(warm[:], 1.0)
         nc.scalar.sqrt(out=warm[:, 1:2], in_=warm[:, 0:1])
 
-        regroup(0)
+        regroup(0, (VECTOR_AND_SCALAR,))
 
         w_grouped = consts.tile([P, GROUPS * P * PACK], BF16, align_bytes=64)
         w_grouped_words = w_grouped[:].bitcast(F32).rearrange("p (g c e) -> p g c e", g=GROUPS, e=2)
@@ -303,7 +311,7 @@ def tile_selfattention_pa_t_kernel(
         w_scales = consts.tile([P, GROUPS * P], U8, align_bytes=64)
         nc.vector.quantize_mx(out=w_codes[:].bitcast(FP8X4), scales=w_scales[:], in_=w_grouped[:])
         multiply(0, (GROUP_Q,))
-        regroup(1)
+        regroup(1, (VECTOR_AND_SCALAR,))
 
         vector_t = psum_one.tile([P, P], BF16, tag="t_v")
         nc.tensor.transpose(out=vector_t[:], in_=vector_rows[:], identity=identity_bf16[:])
@@ -348,11 +356,13 @@ def tile_selfattention_pa_t_kernel(
                 start_windows(step + 1, POOLED_GROUPS[2:])
             if live(step):
                 fold_windows(step)
+            if live(step + LEAD - 1):
+                quantise(step + LEAD - 1)
             if live(step + LEAD):
-                regroup(step + LEAD)
+                regroup(step + LEAD, (VECTOR_AND_SCALAR,))
+            if live(step + LEAD + 1):
+                regroup(step + LEAD + 1, (GPSIMD,))
             if live(step):
                 store_q(step)
             if live(step - 1):
                 store_v(step - 1)
-            if live(step + LEAD - 1):
-                quantise(step + LEAD - 1)

@@ -38,7 +38,7 @@ MEAN = 3
 VARIANCE = 4
 
 HEAD_SPLIT = (64, 128)
-STEP_SPLIT = (40, 64)
+STEP_SPLIT = (48, 80)
 FIRST_SHARED = 3
 VECTOR_AND_SCALAR = 0
 GPSIMD = 1

@@ -20,10 +20,14 @@ EPS = 1e-5
 P = 128
 PACK = 4
 UNIT = 512
+PAIR = 2 * UNIT
 UNITS_PER_IMAGE = POSITIONS // UNIT
+PAIRS_PER_IMAGE = POSITIONS // PAIR
 UNITS = IMAGES * UNITS_PER_IMAGE
-POOLED = UNIT // 4
+WINDOWS = PAIR // 4
+HALF_WIDTH = WIDTH // 2
 RUN = 4
+RUNS = UNIT // RUN
 
 GROUPS = 4
 GROUP_Q = 0
@@ -37,14 +41,23 @@ SHIFT = 2
 MEAN = 3
 VARIANCE = 4
 
-HEAD_SPLIT = (64, 128)
-STEP_SPLIT = (48, 80)
-FIRST_SHARED = 3
-VECTOR_AND_SCALAR = 0
-GPSIMD = 1
 LEAD = 3
 
 FLOPS = 2 * IMAGES * POSITIONS * CHANNELS * GROUPS * P
+
+
+def split_of(unit):
+    if unit == 2:
+        return (64, RUNS)
+    if unit == 3:
+        return (64, 96)
+    if unit % 2 == 0:
+        return SPLIT_EVEN
+    return SPLIT_ODD
+
+
+SPLIT_EVEN = (40, 64)
+SPLIT_ODD = (60, 96)
 
 
 def tile_selfattention_pa_t_kernel(
@@ -61,7 +74,7 @@ def tile_selfattention_pa_t_kernel(
         raws = ctx.enter_context(tc.tile_pool(name="raws", bufs=1))
         stage = ctx.enter_context(tc.tile_pool(name="stage", bufs=2))
         work = ctx.enter_context(tc.tile_pool(name="work", bufs=2))
-        rows = ctx.enter_context(tc.tile_pool(name="rows", bufs=4))
+        rows = ctx.enter_context(tc.tile_pool(name="rows", bufs=3))
         psum_kv = ctx.enter_context(tc.psum_pool(name="psum_kv", bufs=5))
         psum_one = ctx.enter_context(tc.psum_pool(name="psum_one", bufs=1))
         ctx.enter_context(tc.manual_schedule())
@@ -96,15 +109,18 @@ def tile_selfattention_pa_t_kernel(
             small_loads.append((vector_rows[row + 2 : row + 4, :], vec_v.rearrange("(g c) -> g c", g=2)))
 
         mem = memory.rearrange("b (p j) h w -> b p j (h w)", j=PACK)
-        raw_of_unit = []
+        pieces_of_pair = []
+        for pair in range(UNITS // 2):
+            pieces_of_pair.append([])
         vectors_behind = (4, 6, 5)
         for image in range(IMAGES):
-            load_width = UNIT if image == 0 else 2 * UNIT
+            load_width = UNIT if image == 0 else PAIR
             for first in range(0, POSITIONS, load_width):
                 raw = raws.tile([P, PACK, load_width], BF16, name="raw_%d_%d" % (image, first))
                 nc.sync.dma_start(out=raw[:], in_=mem[image, :, :, first : first + load_width])
-                for start in range(0, load_width, UNIT):
-                    raw_of_unit.append(raw[:, :, start : start + UNIT])
+                pieces_of_pair[image * PAIRS_PER_IMAGE + first // PAIR].append(
+                    (raw, (first % PAIR) // 2, load_width // 2)
+                )
                 for dst, src in weight_loads:
                     nc.sync.dma_start(out=dst, in_=src)
                 weight_loads = []
@@ -123,31 +139,51 @@ def tile_selfattention_pa_t_kernel(
         t_q_of = {}
         t_v_of = {}
         k_of = {}
+        q_rows_of = {}
 
-        def split_of(unit):
-            return HEAD_SPLIT if unit < FIRST_SHARED else STEP_SPLIT
-
-        def regroup(unit, engines):
-            split = split_of(unit)
+        def regroup(unit, engine, first_run, end_run):
             if unit not in grouped_of:
                 new_tile = stage.tile([P, UNIT, PACK], BF16, align_bytes=64, tag="grouped")
                 grouped_of[unit] = new_tile
             grouped = grouped_of[unit]
-            dst = grouped[:].rearrange("p (c i) j -> p c j i", i=RUN)
-            src = raw_of_unit[unit].rearrange("p j (c i) -> p c j i", i=RUN)
-            vector_end, scalar_end = split
-            if VECTOR_AND_SCALAR in engines:
-                nc.vector.tensor_copy(out=dst[:, :vector_end], in_=src[:, :vector_end])
-                nc.scalar.copy(out=dst[:, vector_end:scalar_end], in_=src[:, vector_end:scalar_end])
-            if GPSIMD in engines and scalar_end < UNIT // RUN:
+            for raw, piece_first, piece_columns in pieces_of_pair[unit // 2]:
+                lo = max(first_run * RUN, piece_first)
+                hi = min(end_run * RUN, piece_first + piece_columns)
+                if lo < hi:
+                    by_parity = raw[:].rearrange("p j (n b) -> p j n b", b=2)
+                    regroup_columns(
+                        engine, grouped[:, lo:hi, :], by_parity[:, :, lo - piece_first : hi - piece_first, unit % 2]
+                    )
+
+        def regroup_columns(engine, dst, src):
+            if engine == "vector":
+                nc.vector.tensor_copy(
+                    out=dst.rearrange("p (c i) j -> p c j i", i=RUN),
+                    in_=src.rearrange("p j (c i) -> p c j i", i=RUN),
+                )
+            elif engine == "scalar":
+                nc.scalar.copy(
+                    out=dst.rearrange("p (c i) j -> p c j i", i=RUN),
+                    in_=src.rearrange("p j (c i) -> p c j i", i=RUN),
+                )
+            else:
                 nc.gpsimd.tensor_scalar(
-                    out=grouped[:, scalar_end * RUN :, :],
-                    in0=raw_of_unit[unit][:, :, scalar_end * RUN :].rearrange("p j n -> p n j"),
+                    out=dst,
+                    in0=src.rearrange("p j n -> p n j"),
                     scalar1=1.0,
                     scalar2=0.0,
                     op0=ALU.mult,
                     op1=ALU.add,
                 )
+
+        def regroup_vector(unit):
+            regroup(unit, "vector", 0, split_of(unit)[0])
+
+        def regroup_scalar(unit):
+            regroup(unit, "scalar", split_of(unit)[0], split_of(unit)[1])
+
+        def regroup_gpsimd(unit):
+            regroup(unit, "gpsimd", split_of(unit)[1], RUNS)
 
         def quantise(unit):
             nc.vector.quantize_mx(
@@ -184,52 +220,57 @@ def tile_selfattention_pa_t_kernel(
             )
             z_q_of[unit] = z_q
 
-        def member(unit, group, a, b):
-            windows = sums_of[(unit, group)][:].rearrange(
-                "c (hh a ww b) -> c a b hh ww", a=2, ww=WIDTH // 2, b=2
-            )
-            return windows[:, a, b]
+        def member(unit, group, a):
+            by_row = sums_of[(unit, group)][:].rearrange("c (hh a ww) -> c a hh ww", a=2, ww=HALF_WIDTH)
+            return by_row[:, a]
 
-        def peak_view(unit, group):
-            return peak_of[unit][:, group - 1, :].rearrange("c (hh ww) -> c hh ww", ww=WIDTH // 2)
+        def by_window_row(flat):
+            return flat.rearrange("c (hh ww) -> c hh ww", ww=HALF_WIDTH)
+
+        def peak_view(pair, group):
+            return by_window_row(peak_of[pair][:, group - 1, :])
 
         def start_windows(unit, groups):
-            if unit not in peak_of:
-                peak = work.tile([P, len(POOLED_GROUPS), POOLED], F32)
-                peak_of[unit] = peak
+            pair = unit // 2
+            if pair not in peak_of:
+                peak = work.tile([P, len(POOLED_GROUPS), WINDOWS], F32)
+                peak_of[pair] = peak
             for group in groups:
                 nc.scalar.activation(
-                    out=peak_view(unit, group),
-                    in_=member(unit, group, 0, 0),
+                    out=peak_view(pair, group),
+                    in_=member(unit, group, 0),
                     func=ACT.Copy,
                     scale=inv[:, group : group + 1],
                 )
 
         def fold_windows(unit):
-            image = unit // UNITS_PER_IMAGE
-            unit_in_image = unit % UNITS_PER_IMAGE
-            if unit_in_image == 0:
-                k_image = work.tile([P, UNITS_PER_IMAGE, POOLED], F32)
-                k_of[image] = k_image
-            z_v = work.tile([P, 2, POOLED], F32)
-            z_v_of[unit] = z_v
-            finished = (k_of[image][:, unit_in_image, :], z_v[:, 0, :], z_v[:, 1, :])
-            for a, b in ((0, 1), (1, 0), (1, 1)):
+            pair = unit // 2
+            image = pair // PAIRS_PER_IMAGE
+            pair_in_image = pair % PAIRS_PER_IMAGE
+            odd = unit % 2 == 1
+            if odd:
+                if pair_in_image == 0:
+                    k_image = work.tile([P, PAIRS_PER_IMAGE, WINDOWS], F32)
+                    k_of[image] = k_image
+                z_v = work.tile([P, 2, WINDOWS], F32)
+                z_v_of[pair] = z_v
+                finished = (k_of[image][:, pair_in_image, :], z_v[:, 0, :], z_v[:, 1, :])
+            for a in (0, 1) if odd else (1,):
                 for group in POOLED_GROUPS:
-                    if (a, b) == (1, 1):
-                        target = finished[group - 1].rearrange("c (hh ww) -> c hh ww", ww=WIDTH // 2)
+                    if odd and a == 1:
+                        target = by_window_row(finished[group - 1])
                     else:
-                        target = peak_view(unit, group)
+                        target = peak_view(pair, group)
                     nc.vector.scalar_tensor_tensor(
                         out=target,
-                        in0=member(unit, group, a, b),
+                        in0=member(unit, group, a),
                         scalar=inv[:, group : group + 1],
-                        in1=peak_view(unit, group),
+                        in1=peak_view(pair, group),
                         op0=ALU.mult,
                         op1=ALU.max,
                     )
-            if unit_in_image == UNITS_PER_IMAGE - 1:
-                k_rows = work.tile([P, UNITS_PER_IMAGE * POOLED], F32)
+            if odd and pair_in_image == PAIRS_PER_IMAGE - 1:
+                k_rows = work.tile([P, PAIRS_PER_IMAGE * WINDOWS], F32)
                 nc.vector.tensor_scalar_add(
                     out=k_rows[:],
                     in0=k_of[image][:].rearrange("c u n -> c (u n)"),
@@ -243,8 +284,12 @@ def tile_selfattention_pa_t_kernel(
                 nc.tensor.transpose(out=t_q[:, i, :], in_=z_q_of[unit][:, i, :], identity=identity[:])
             t_q_of[unit] = t_q
 
-        def transpose_v(unit):
-            t_v = psum_one.tile([P, 2, P], F32, tag="t_v")
+        def transpose_v(block):
+            if block == UNITS - 1:
+                t_v = psum_kv.tile([P, 2, P], F32, tag="acc_kv")
+            else:
+                t_v = psum_one.tile([P, 2, P], F32, tag="t_v")
+            first = (block % 2) * P
             for half in range(2):
                 group = POOLED_GROUPS[1 + half]
                 nc.tensor.matmul(
@@ -257,32 +302,38 @@ def tile_selfattention_pa_t_kernel(
                 )
                 nc.tensor.matmul(
                     out=t_v[:, half, :],
-                    lhsT=z_v_of[unit][:, half, :],
+                    lhsT=z_v_of[block // 2][:, half, first : first + P],
                     rhs=identity[:],
                     is_transpose=True,
                     start=False,
                     stop=True,
                 )
-            t_v_of[unit] = t_v
+            t_v_of[block] = t_v
 
         def store_q(unit):
-            q_rows = rows.tile([P, PACK, P], F32)
-            nc.scalar.copy(out=q_rows[:], in_=t_q_of[unit][:])
-            first = (unit % UNITS_PER_IMAGE) * UNIT
-            nc.sync.dma_start(
-                out=out_q[unit // UNITS_PER_IMAGE, first : first + UNIT, :].rearrange("(r i) c -> r i c", i=PACK),
-                in_=q_rows[:],
-            )
+            pair = unit // 2
+            if pair not in q_rows_of:
+                q_rows = rows.tile([P, PACK, 2, P], F32)
+                q_rows_of[pair] = q_rows
+            nc.scalar.copy(out=q_rows_of[pair][:, :, unit % 2, :], in_=t_q_of[unit][:])
+            if unit % 2 == 1:
+                first = (pair % PAIRS_PER_IMAGE) * PAIR
+                nc.sync.dma_start(
+                    out=out_q[pair // PAIRS_PER_IMAGE, first : first + PAIR, :].rearrange(
+                        "(r i b) c -> r i b c", i=PACK, b=2
+                    ),
+                    in_=q_rows_of[pair][:],
+                )
 
-        def store_v(unit):
+        def store_v(block):
             v_rows = rows.tile([P, 2, P], F32)
-            if unit < UNITS - 2:
-                nc.scalar.copy(out=v_rows[:], in_=t_v_of[unit][:])
+            if block == UNITS - 2:
+                nc.vector.tensor_copy(out=v_rows[:], in_=t_v_of[block][:])
             else:
-                nc.vector.tensor_copy(out=v_rows[:], in_=t_v_of[unit][:])
-            first = (unit % UNITS_PER_IMAGE) * POOLED
+                nc.scalar.copy(out=v_rows[:], in_=t_v_of[block][:])
+            first = (block % UNITS_PER_IMAGE) * P
             nc.sync.dma_start(
-                out=out_v[unit // UNITS_PER_IMAGE, first : first + POOLED, :].rearrange("n (h c) -> n h c", h=2),
+                out=out_v[block // UNITS_PER_IMAGE, first : first + P, :].rearrange("n (h c) -> n h c", h=2),
                 in_=v_rows[:],
             )
 
@@ -290,7 +341,8 @@ def tile_selfattention_pa_t_kernel(
         nc.vector.memset(warm[:], 1.0)
         nc.scalar.sqrt(out=warm[:, 1:2], in_=warm[:, 0:1])
 
-        regroup(0, (VECTOR_AND_SCALAR,))
+        regroup(0, "vector", 0, RUNS // 2)
+        regroup(1, "scalar", 0, RUNS // 2)
 
         w_grouped = consts.tile([P, GROUPS * P * PACK], BF16, align_bytes=64)
         w_grouped_words = w_grouped[:].bitcast(F32).rearrange("p (g c e) -> p g c e", g=GROUPS, e=2)
@@ -306,12 +358,13 @@ def tile_selfattention_pa_t_kernel(
                 )
             else:
                 nc.scalar.copy(out=w_grouped_words[:, 2:4, :, :], in_=w_t[:].rearrange("p g e c -> p g c e"))
-        quantise(0)
         w_codes = consts.tile([P, GROUPS * P], U32, align_bytes=64)
         w_scales = consts.tile([P, GROUPS * P], U8, align_bytes=64)
         nc.vector.quantize_mx(out=w_codes[:].bitcast(FP8X4), scales=w_scales[:], in_=w_grouped[:])
+        regroup(0, "vector", RUNS // 2, RUNS)
+        regroup(1, "scalar", RUNS // 2, RUNS)
+        quantise(0)
         multiply(0, (GROUP_Q,))
-        regroup(1, (VECTOR_AND_SCALAR,))
 
         vector_t = psum_one.tile([P, P], BF16, tag="t_v")
         nc.tensor.transpose(out=vector_t[:], in_=vector_rows[:], identity=identity_bf16[:])
@@ -342,27 +395,32 @@ def tile_selfattention_pa_t_kernel(
         def live(unit):
             return 0 <= unit < UNITS
 
-        for step in range(-1, UNITS + 2):
+        for step in range(-1, UNITS + 1):
             if step >= 0 and live(step + 1):
                 multiply(step + 1, range(GROUPS))
             if live(step):
                 transpose_q(step)
-            if live(step - 1):
-                transpose_v(step - 1)
+            blocks = (UNITS - 2, UNITS - 1) if step == UNITS else (step - 2,)
+            for block in blocks:
+                if live(block):
+                    transpose_v(block)
             if live(step + 1):
-                start_windows(step + 1, POOLED_GROUPS[:2])
+                if (step + 1) % 2 == 0:
+                    start_windows(step + 1, POOLED_GROUPS[:2])
                 normalise_q(step + 1)
-            if live(step + 1):
-                start_windows(step + 1, POOLED_GROUPS[2:])
+                if (step + 1) % 2 == 0:
+                    start_windows(step + 1, POOLED_GROUPS[2:])
             if live(step):
                 fold_windows(step)
             if live(step + LEAD - 1):
                 quantise(step + LEAD - 1)
             if live(step + LEAD):
-                regroup(step + LEAD, (VECTOR_AND_SCALAR,))
+                regroup_vector(step + LEAD)
+                regroup_scalar(step + LEAD)
             if live(step + LEAD + 1):
-                regroup(step + LEAD + 1, (GPSIMD,))
+                regroup_gpsimd(step + LEAD + 1)
             if live(step):
                 store_q(step)
-            if live(step - 1):
-                store_v(step - 1)
+            for block in blocks:
+                if live(block):
+                    store_v(block)

@@ -26,6 +26,8 @@ PAIRS_PER_IMAGE = POSITIONS // PAIR
 UNITS = IMAGES * UNITS_PER_IMAGE
 WINDOWS = PAIR // 4
 HALF_WIDTH = WIDTH // 2
+WINDOW_ROWS = WINDOWS // HALF_WIDTH
+BLOCK_ROWS = P // HALF_WIDTH
 RUN = 4
 RUNS = UNIT // RUN
 
@@ -41,15 +43,18 @@ SHIFT = 2
 MEAN = 3
 VARIANCE = 4
 
+NEEDS = 3
+NEED_SCALE_KV = 0
+NEED_Q = 1
+NEED_ADDEND_KV = 2
+
 LEAD = 3
 
 FLOPS = 2 * IMAGES * POSITIONS * CHANNELS * GROUPS * P
 
 
 def split_of(unit):
-    if unit == 2:
-        return (64, RUNS)
-    if unit == 3:
+    if unit < UNITS_PER_IMAGE:
         return (64, 96)
     if unit % 2 == 0:
         return SPLIT_EVEN
@@ -85,15 +90,11 @@ def tile_selfattention_pa_t_kernel(
         make_identity(nc, identity_bf16[:])
 
         w_rows = consts.tile([P, GROUPS, CHANNELS], BF16)
-        vector_rows = consts.tile([P, P], BF16)
-        nc.vector.memset(vector_rows[:], 0.0)
-
-        weight_loads = [
-            (w_rows[:, 0, :], wq),
-            (w_rows[:, 1, :], wk),
-            (w_rows[:, 2:4, :], wv.rearrange("(g c) k -> c g k", g=2)),
-        ]
-        small_loads = []
+        tables = []
+        for need in range(NEEDS):
+            table = consts.tile([P, P], BF16, name="table_%d" % need)
+            nc.vector.memset(table[:], 0.0)
+            tables.append(table)
         vectors_of_kind = (
             (bq, bk, bv),
             (bnq_s, bnk_s, bnv_s),
@@ -101,33 +102,42 @@ def tile_selfattention_pa_t_kernel(
             (bnq_m, bnk_m, bnv_m),
             (bnq_v, bnk_v, bnv_v),
         )
-        for kind in range(KINDS):
-            vec_q, vec_k, vec_v = vectors_of_kind[kind]
-            row = GROUPS * kind
-            small_loads.append((vector_rows[row : row + 1, :], vec_q.rearrange("(g c) -> g c", g=1)))
-            small_loads.append((vector_rows[row + 1 : row + 2, :], vec_k.rearrange("(g c) -> g c", g=1)))
-            small_loads.append((vector_rows[row + 2 : row + 4, :], vec_v.rearrange("(g c) -> g c", g=2)))
+
+        def load_vector(need, kind, who):
+            row = GROUPS * kind + who
+            groups = 2 if who == 2 else 1
+            nc.sync.dma_start(
+                out=tables[need][row : row + groups, :],
+                in_=vectors_of_kind[kind][who].rearrange("(g c) -> g c", g=groups),
+            )
 
         mem = memory.rearrange("b (p j) h w -> b p j (h w)", j=PACK)
         pieces_of_pair = []
         for pair in range(UNITS // 2):
             pieces_of_pair.append([])
-        vectors_behind = (4, 6, 5)
-        for image in range(IMAGES):
-            load_width = UNIT if image == 0 else PAIR
-            for first in range(0, POSITIONS, load_width):
-                raw = raws.tile([P, PACK, load_width], BF16, name="raw_%d_%d" % (image, first))
-                nc.sync.dma_start(out=raw[:], in_=mem[image, :, :, first : first + load_width])
-                pieces_of_pair[image * PAIRS_PER_IMAGE + first // PAIR].append(
-                    (raw, (first % PAIR) // 2, load_width // 2)
-                )
-                for dst, src in weight_loads:
-                    nc.sync.dma_start(out=dst, in_=src)
-                weight_loads = []
-                for dst, src in small_loads[: vectors_behind[0]]:
-                    nc.sync.dma_start(out=dst, in_=src)
-                small_loads = small_loads[vectors_behind[0] :]
-                vectors_behind = vectors_behind[1:] + (0,)
+
+        def load_memory(image, first, load_width):
+            raw = raws.tile([P, PACK, load_width], BF16, name="raw_%d_%d" % (image, first))
+            nc.sync.dma_start(out=raw[:], in_=mem[image, :, :, first : first + load_width])
+            pieces_of_pair[image * PAIRS_PER_IMAGE + first // PAIR].append((raw, (first % PAIR) // 2, load_width // 2))
+
+        load_memory(0, 0, UNIT)
+        nc.sync.dma_start(out=w_rows[:, 0, :], in_=wq)
+        nc.sync.dma_start(out=w_rows[:, 1, :], in_=wk)
+        nc.sync.dma_start(out=w_rows[:, 2:4, :], in_=wv.rearrange("(g c) k -> c g k", g=2))
+        load_memory(0, UNIT, UNIT)
+        for kind, who in ((GAIN, 2), (VARIANCE, 2), (GAIN, 1), (VARIANCE, 1)):
+            load_vector(NEED_SCALE_KV, kind, who)
+        for kind in (VARIANCE, GAIN, BIAS, MEAN, SHIFT):
+            load_vector(NEED_Q, kind, 0)
+        load_memory(0, 2 * UNIT, UNIT)
+        load_memory(0, 3 * UNIT, UNIT)
+        for kind in (BIAS, MEAN, SHIFT):
+            for who in (1, 2):
+                load_vector(NEED_ADDEND_KV, kind, who)
+        for image in range(1, IMAGES):
+            for first in range(0, POSITIONS, PAIR):
+                load_memory(image, first, PAIR)
 
         mem_codes = consts.tile([P, UNITS, UNIT], U32, align_bytes=64)
         mem_scales = consts.tile([P, UNITS, UNIT], U8, align_bytes=64)
@@ -255,28 +265,43 @@ def tile_selfattention_pa_t_kernel(
                 z_v = work.tile([P, 2, WINDOWS], F32)
                 z_v_of[pair] = z_v
                 finished = (k_of[image][:, pair_in_image, :], z_v[:, 0, :], z_v[:, 1, :])
-            for a in (0, 1) if odd else (1,):
-                for group in POOLED_GROUPS:
-                    if odd and a == 1:
-                        target = by_window_row(finished[group - 1])
-                    else:
-                        target = peak_view(pair, group)
-                    nc.vector.scalar_tensor_tensor(
-                        out=target,
-                        in0=member(unit, group, a),
-                        scalar=inv[:, group : group + 1],
-                        in1=peak_view(pair, group),
-                        op0=ALU.mult,
-                        op1=ALU.max,
-                    )
-            if odd and pair_in_image == PAIRS_PER_IMAGE - 1:
-                k_rows = work.tile([P, PAIRS_PER_IMAGE * WINDOWS], F32)
+            every_row = slice(0, WINDOW_ROWS)
+            turns = []
+            if odd:
+                turns.extend([(group, 0, every_row) for group in POOLED_GROUPS])
+            if unit < UNITS - 1:
+                turns.extend([(group, 1, every_row) for group in POOLED_GROUPS])
+            else:
+                for first_row in range(0, WINDOW_ROWS, BLOCK_ROWS):
+                    turns.extend([(group, 1, slice(first_row, first_row + BLOCK_ROWS)) for group in POOLED_GROUPS[1:]])
+                turns.append((GROUP_K, 1, every_row))
+            for group, a, window_rows in turns:
+                if odd and a == 1:
+                    target = by_window_row(finished[group - 1])
+                else:
+                    target = peak_view(pair, group)
+                nc.vector.scalar_tensor_tensor(
+                    out=target[:, window_rows, :],
+                    in0=member(unit, group, a)[:, window_rows, :],
+                    scalar=inv[:, group : group + 1],
+                    in1=peak_view(pair, group)[:, window_rows, :],
+                    op0=ALU.mult,
+                    op1=ALU.max,
+                )
+            if image == IMAGES - 1:
+                first_pair = pair_in_image
+            else:
+                first_pair = 0
+            if odd and (image == IMAGES - 1 or pair_in_image == PAIRS_PER_IMAGE - 1):
+                k_rows = work.tile([P, (pair_in_image + 1 - first_pair) * WINDOWS], F32)
                 nc.vector.tensor_scalar_add(
                     out=k_rows[:],
-                    in0=k_of[image][:].rearrange("c u n -> c (u n)"),
+                    in0=k_of[image][:, first_pair : pair_in_image + 1, :].rearrange("c u n -> c (u n)"),
                     scalar1=addend[:, GROUP_K : GROUP_K + 1],
                 )
-                nc.sync.dma_start(out=out_k[image], in_=k_rows[:])
+                nc.sync.dma_start(
+                    out=out_k[image, :, first_pair * WINDOWS : (pair_in_image + 1) * WINDOWS], in_=k_rows[:]
+                )
 
         def transpose_q(unit):
             t_q = psum_one.tile([P, PACK, P], F32, tag="t_q")
@@ -284,31 +309,31 @@ def tile_selfattention_pa_t_kernel(
                 nc.tensor.transpose(out=t_q[:, i, :], in_=z_q_of[unit][:, i, :], identity=identity[:])
             t_q_of[unit] = t_q
 
-        def transpose_v(block):
-            if block == UNITS - 1:
-                t_v = psum_kv.tile([P, 2, P], F32, tag="acc_kv")
+        def transpose_v(pair, blocks):
+            if len(blocks) == 2:
+                t_v = psum_one.tile([P, 2, 2, P], F32, tag="t_v")
             else:
-                t_v = psum_one.tile([P, 2, P], F32, tag="t_v")
-            first = (block % 2) * P
-            for half in range(2):
-                group = POOLED_GROUPS[1 + half]
-                nc.tensor.matmul(
-                    out=t_v[:, half, :],
-                    lhsT=addend[:, group : group + 1].to_broadcast([P, P]),
-                    rhs=identity[:],
-                    is_transpose=True,
-                    start=True,
-                    stop=False,
-                )
-                nc.tensor.matmul(
-                    out=t_v[:, half, :],
-                    lhsT=z_v_of[block // 2][:, half, first : first + P],
-                    rhs=identity[:],
-                    is_transpose=True,
-                    start=False,
-                    stop=True,
-                )
-            t_v_of[block] = t_v
+                t_v = psum_kv.tile([P, 1, 2, P], F32, tag="acc_kv")
+            for slot, block in enumerate(blocks):
+                for half in range(2):
+                    group = POOLED_GROUPS[1 + half]
+                    nc.tensor.matmul(
+                        out=t_v[:, slot, half, :],
+                        lhsT=addend[:, group : group + 1].to_broadcast([P, P]),
+                        rhs=identity[:],
+                        is_transpose=True,
+                        start=True,
+                        stop=False,
+                    )
+                    nc.tensor.matmul(
+                        out=t_v[:, slot, half, :],
+                        lhsT=z_v_of[pair][:, half, block * P : (block + 1) * P],
+                        rhs=identity[:],
+                        is_transpose=True,
+                        start=False,
+                        stop=True,
+                    )
+            t_v_of[(pair, blocks)] = t_v
 
         def store_q(unit):
             pair = unit // 2
@@ -316,24 +341,26 @@ def tile_selfattention_pa_t_kernel(
                 q_rows = rows.tile([P, PACK, 2, P], F32)
                 q_rows_of[pair] = q_rows
             nc.scalar.copy(out=q_rows_of[pair][:, :, unit % 2, :], in_=t_q_of[unit][:])
-            if unit % 2 == 1:
-                first = (pair % PAIRS_PER_IMAGE) * PAIR
-                nc.sync.dma_start(
-                    out=out_q[pair // PAIRS_PER_IMAGE, first : first + PAIR, :].rearrange(
-                        "(r i b) c -> r i b c", i=PACK, b=2
-                    ),
-                    in_=q_rows_of[pair][:],
-                )
+            first = (pair % PAIRS_PER_IMAGE) * PAIR
+            q_of_pair = out_q[pair // PAIRS_PER_IMAGE, first : first + PAIR, :].rearrange(
+                "(r i b) c -> r i b c", i=PACK, b=2
+            )
+            if pair == UNITS // 2 - 1:
+                nc.sync.dma_start(out=q_of_pair[:, :, unit % 2, :], in_=q_rows_of[pair][:, :, unit % 2, :])
+            elif unit % 2 == 1:
+                nc.sync.dma_start(out=q_of_pair, in_=q_rows_of[pair][:])
 
-        def store_v(block):
-            v_rows = rows.tile([P, 2, P], F32)
-            if block == UNITS - 2:
-                nc.vector.tensor_copy(out=v_rows[:], in_=t_v_of[block][:])
+        def store_v(pair, blocks, engine):
+            v_rows = rows.tile([P, len(blocks), 2, P], F32)
+            if engine == "vector":
+                nc.vector.tensor_copy(out=v_rows[:], in_=t_v_of[(pair, blocks)][:])
             else:
-                nc.scalar.copy(out=v_rows[:], in_=t_v_of[block][:])
-            first = (block % UNITS_PER_IMAGE) * P
+                nc.scalar.copy(out=v_rows[:], in_=t_v_of[(pair, blocks)][:])
+            first = (pair % PAIRS_PER_IMAGE) * WINDOWS + blocks[0] * P
             nc.sync.dma_start(
-                out=out_v[block // UNITS_PER_IMAGE, first : first + P, :].rearrange("n (h c) -> n h c", h=2),
+                out=out_v[pair // PAIRS_PER_IMAGE, first : first + len(blocks) * P, :].rearrange(
+                    "(e n) (h c) -> n e h c", e=len(blocks), h=2
+                ),
                 in_=v_rows[:],
             )
 
@@ -360,37 +387,52 @@ def tile_selfattention_pa_t_kernel(
                 nc.scalar.copy(out=w_grouped_words[:, 2:4, :, :], in_=w_t[:].rearrange("p g e c -> p g c e"))
         w_codes = consts.tile([P, GROUPS * P], U32, align_bytes=64)
         w_scales = consts.tile([P, GROUPS * P], U8, align_bytes=64)
-        nc.vector.quantize_mx(out=w_codes[:].bitcast(FP8X4), scales=w_scales[:], in_=w_grouped[:])
+
+        def quantise_weights(half):
+            columns = slice(half * 2 * P, (half + 1) * 2 * P)
+            nc.vector.quantize_mx(
+                out=w_codes[:, columns].bitcast(FP8X4),
+                scales=w_scales[:, columns],
+                in_=w_grouped[:, half * 2 * P * PACK : (half + 1) * 2 * P * PACK],
+            )
+
+        quantise_weights(0)
         regroup(0, "vector", RUNS // 2, RUNS)
         regroup(1, "scalar", RUNS // 2, RUNS)
+        quantise_weights(1)
         quantise(0)
-        multiply(0, (GROUP_Q,))
+        regroup_gpsimd(2)
 
-        vector_t = psum_one.tile([P, P], BF16, tag="t_v")
-        nc.tensor.transpose(out=vector_t[:], in_=vector_rows[:], identity=identity_bf16[:])
-        multiply(0, POOLED_GROUPS)
-        deviation = consts.tile([P, GROUPS], F32)
-        nc.scalar.activation(
-            out=deviation[:],
-            in_=vector_t[:, VARIANCE * GROUPS : (VARIANCE + 1) * GROUPS],
-            func=ACT.Sqrt,
-            bias=EPS,
-        )
-        per_channel = consts.tile([P, KINDS, GROUPS], F32)
-        nc.vector.tensor_copy(
-            out=per_channel[:],
-            in_=vector_t[:, 0 : KINDS * GROUPS].rearrange("p (k g) -> p k g", g=GROUPS),
-        )
-        inv_deviation = consts.tile([P, GROUPS], F32)
-        nc.vector.reciprocal(out=inv_deviation[:], in_=deviation[:])
         inv = consts.tile([P, GROUPS], F32)
-        nc.vector.tensor_mul(out=inv[:], in0=per_channel[:, GAIN, :], in1=inv_deviation[:])
-        centred = consts.tile([P, GROUPS], F32)
-        nc.vector.tensor_sub(out=centred[:], in0=per_channel[:, BIAS, :], in1=per_channel[:, MEAN, :])
-        centred_scaled = consts.tile([P, GROUPS], F32)
-        nc.vector.tensor_mul(out=centred_scaled[:], in0=centred[:], in1=inv[:])
         addend = consts.tile([P, GROUPS], F32)
-        nc.vector.tensor_add(out=addend[:], in0=centred_scaled[:], in1=per_channel[:, SHIFT, :])
+        deviation = consts.tile([P, GROUPS], F32)
+        inv_deviation = consts.tile([P, GROUPS], F32)
+        centred = consts.tile([P, GROUPS], F32)
+        own = consts.tile([P, KINDS, GROUPS], F32)
+
+        def transposed_table(need, tag):
+            table_t = psum_one.tile([P, P], BF16, tag=tag)
+            nc.tensor.transpose(out=table_t[:], in_=tables[need][:], identity=identity_bf16[:])
+            return table_t[:, 0 : KINDS * GROUPS].rearrange("p (k g) -> p k g", g=GROUPS)
+
+        def make_inv(values, groups):
+            nc.scalar.activation(out=deviation[:, groups], in_=values[:, VARIANCE, groups], func=ACT.Sqrt, bias=EPS)
+            nc.vector.reciprocal(out=inv_deviation[:, groups], in_=deviation[:, groups])
+            nc.vector.tensor_mul(out=inv[:, groups], in0=values[:, GAIN, groups], in1=inv_deviation[:, groups])
+
+        def make_addend(values, groups):
+            nc.vector.tensor_copy(out=own[:, BIAS : MEAN + 1, groups], in_=values[:, BIAS : MEAN + 1, groups])
+            nc.vector.tensor_sub(out=centred[:, groups], in0=own[:, BIAS, groups], in1=own[:, MEAN, groups])
+            nc.vector.tensor_mul(out=centred[:, groups], in0=centred[:, groups], in1=inv[:, groups])
+            nc.vector.tensor_add(out=addend[:, groups], in0=centred[:, groups], in1=own[:, SHIFT, groups])
+
+        pooled = slice(GROUP_K, GROUPS)
+        only_q = slice(GROUP_Q, GROUP_Q + 1)
+        make_inv(transposed_table(NEED_SCALE_KV, "t_v"), pooled)
+        values_q = transposed_table(NEED_Q, "t_q")
+        make_inv(values_q, only_q)
+        make_addend(values_q, only_q)
+        multiply(0, range(GROUPS))
 
         def live(unit):
             return 0 <= unit < UNITS
@@ -400,10 +442,13 @@ def tile_selfattention_pa_t_kernel(
                 multiply(step + 1, range(GROUPS))
             if live(step):
                 transpose_q(step)
-            blocks = (UNITS - 2, UNITS - 1) if step == UNITS else (step - 2,)
-            for block in blocks:
-                if live(block):
-                    transpose_v(block)
+            v_turns = []
+            if step == UNITS:
+                v_turns = [(step // 2 - 1, (0,), "vector"), (step // 2 - 1, (1,), "scalar")]
+            elif step >= 2 and step % 2 == 0:
+                v_turns = [(step // 2 - 1, (0, 1), "scalar")]
+            for pair, blocks, engine in v_turns:
+                transpose_v(pair, blocks)
             if live(step + 1):
                 if (step + 1) % 2 == 0:
                     start_windows(step + 1, POOLED_GROUPS[:2])
@@ -419,8 +464,9 @@ def tile_selfattention_pa_t_kernel(
                 regroup_scalar(step + LEAD)
             if live(step + LEAD + 1):
                 regroup_gpsimd(step + LEAD + 1)
+            if step == 1:
+                make_addend(transposed_table(NEED_ADDEND_KV, "t_v"), pooled)
             if live(step):
                 store_q(step)
-            for block in blocks:
-                if live(block):
-                    store_v(block)
+            for pair, blocks, engine in v_turns:
+                store_v(pair, blocks, engine)

@@ -401,44 +401,65 @@ def tile_selfattention_pa_t_kernel(
         regroup(1, "scalar", RUNS // 2, RUNS)
         quantise_weights(1)
         quantise(0)
-        regroup_gpsimd(2)
 
         inv = consts.tile([P, GROUPS], F32)
         addend = consts.tile([P, GROUPS], F32)
         deviation = consts.tile([P, GROUPS], F32)
         inv_deviation = consts.tile([P, GROUPS], F32)
         centred = consts.tile([P, GROUPS], F32)
-        own = consts.tile([P, KINDS, GROUPS], F32)
+        scaled = consts.tile([P, GROUPS], F32)
+        own_of = {}
 
-        def transposed_table(need, tag):
+        def fetch_table(need, tag, groups, with_variance):
             table_t = psum_one.tile([P, P], BF16, tag=tag)
             nc.tensor.transpose(out=table_t[:], in_=tables[need][:], identity=identity_bf16[:])
-            return table_t[:, 0 : KINDS * GROUPS].rearrange("p (k g) -> p k g", g=GROUPS)
+            values = table_t[:, 0 : KINDS * GROUPS].rearrange("p (k g) -> p k g", g=GROUPS)
+            if with_variance:
+                nc.scalar.activation(
+                    out=deviation[:, groups], in_=values[:, VARIANCE, groups], func=ACT.Sqrt, bias=EPS
+                )
+            own = consts.tile([P, KINDS, GROUPS], F32, name="own_%d" % need)
+            nc.scalar.copy(out=own[:, BIAS : MEAN + 1, :], in_=values[:, BIAS : MEAN + 1, :])
+            own_of[need] = own
 
-        def make_inv(values, groups):
-            nc.scalar.activation(out=deviation[:, groups], in_=values[:, VARIANCE, groups], func=ACT.Sqrt, bias=EPS)
+        def invert(groups):
             nc.vector.reciprocal(out=inv_deviation[:, groups], in_=deviation[:, groups])
-            nc.vector.tensor_mul(out=inv[:, groups], in0=values[:, GAIN, groups], in1=inv_deviation[:, groups])
 
-        def make_addend(values, groups):
-            nc.vector.tensor_copy(out=own[:, BIAS : MEAN + 1, groups], in_=values[:, BIAS : MEAN + 1, groups])
-            nc.vector.tensor_sub(out=centred[:, groups], in0=own[:, BIAS, groups], in1=own[:, MEAN, groups])
-            nc.vector.tensor_mul(out=centred[:, groups], in0=centred[:, groups], in1=inv[:, groups])
-            nc.vector.tensor_add(out=addend[:, groups], in0=centred[:, groups], in1=own[:, SHIFT, groups])
+        def make_inv(need, groups):
+            nc.gpsimd.tensor_mul(out=inv[:, groups], in0=own_of[need][:, GAIN, groups], in1=inv_deviation[:, groups])
+
+        def centre(need, groups):
+            own = own_of[need]
+            nc.gpsimd.tensor_sub(out=centred[:, groups], in0=own[:, BIAS, groups], in1=own[:, MEAN, groups])
+
+        def make_addend(need, groups):
+            nc.gpsimd.tensor_mul(out=scaled[:, groups], in0=centred[:, groups], in1=inv[:, groups])
+            nc.gpsimd.tensor_add(out=addend[:, groups], in0=scaled[:, groups], in1=own_of[need][:, SHIFT, groups])
 
         pooled = slice(GROUP_K, GROUPS)
         only_q = slice(GROUP_Q, GROUP_Q + 1)
-        make_inv(transposed_table(NEED_SCALE_KV, "t_v"), pooled)
-        values_q = transposed_table(NEED_Q, "t_q")
-        make_inv(values_q, only_q)
-        make_addend(values_q, only_q)
+        fetch_table(NEED_SCALE_KV, "t_v", pooled, True)
+        invert(pooled)
+        make_inv(NEED_SCALE_KV, pooled)
+        fetch_table(NEED_Q, "t_q", only_q, True)
+        centre(NEED_Q, only_q)
         multiply(0, range(GROUPS))
+        start_windows(0, POOLED_GROUPS)
+        quantise(1)
+        invert(only_q)
+        make_inv(NEED_Q, only_q)
+        make_addend(NEED_Q, only_q)
+        normalise_q(0)
+        regroup_vector(2)
+        regroup_scalar(2)
+        regroup_gpsimd(2)
+        regroup_gpsimd(3)
 
         def live(unit):
             return 0 <= unit < UNITS
 
-        for step in range(-1, UNITS + 1):
-            if step >= 0 and live(step + 1):
+        for step in range(UNITS + 1):
+            if live(step + 1):
                 multiply(step + 1, range(GROUPS))
             if live(step):
                 transpose_q(step)
@@ -465,7 +486,9 @@ def tile_selfattention_pa_t_kernel(
             if live(step + LEAD + 1):
                 regroup_gpsimd(step + LEAD + 1)
             if step == 1:
-                make_addend(transposed_table(NEED_ADDEND_KV, "t_v"), pooled)
+                fetch_table(NEED_ADDEND_KV, "t_v", pooled, False)
+                centre(NEED_ADDEND_KV, pooled)
+                make_addend(NEED_ADDEND_KV, pooled)
             if live(step):
                 store_q(step)
             for pair, blocks, engine in v_turns:

@@ -458,18 +458,21 @@ def tile_selfattention_pa_t_kernel(
         def live(unit):
             return 0 <= unit < UNITS
 
+        both = (0, 1)
         for step in range(UNITS + 1):
+            if 4 <= step <= UNITS - 2 and step % 2 == 0:
+                store_v((step - 4) // 2, both, "scalar")
             if live(step + 1):
                 multiply(step + 1, range(GROUPS))
             if live(step):
                 transpose_q(step)
-            v_turns = []
+            if 3 <= step < UNITS - 2 and step % 2 == 1:
+                transpose_v((step - 3) // 2, both)
+            if step == UNITS - 2:
+                transpose_v(step // 2 - 1, both)
             if step == UNITS:
-                v_turns = [(step // 2 - 1, (0,), "vector"), (step // 2 - 1, (1,), "scalar")]
-            elif step >= 2 and step % 2 == 0:
-                v_turns = [(step // 2 - 1, (0, 1), "scalar")]
-            for pair, blocks, engine in v_turns:
-                transpose_v(pair, blocks)
+                transpose_v(step // 2 - 1, (0,))
+                transpose_v(step // 2 - 1, (1,))
             if live(step + 1):
                 if (step + 1) % 2 == 0:
                     start_windows(step + 1, POOLED_GROUPS[:2])
@@ -491,5 +494,8 @@ def tile_selfattention_pa_t_kernel(
                 make_addend(NEED_ADDEND_KV, pooled)
             if live(step):
                 store_q(step)
-            for pair, blocks, engine in v_turns:
-                store_v(pair, blocks, engine)
+            if step == UNITS - 2:
+                store_v(step // 2 - 1, both, "scalar")
+            if step == UNITS:
+                store_v(step // 2 - 1, (0,), "vector")
+                store_v(step // 2 - 1, (1,), "scalar")

@@ -61,8 +61,8 @@ def split_of(unit):
     return SPLIT_ODD
 
 
-SPLIT_EVEN = (40, 64)
-SPLIT_ODD = (60, 96)
+SPLIT_EVEN = (48, 80)
+SPLIT_ODD = (64, 108)
 
 
 def tile_selfattention_pa_t_kernel(

@@ -54,15 +54,17 @@ FLOPS = 2 * IMAGES * POSITIONS * CHANNELS * GROUPS * P
 
 
 def split_of(unit):
-    if unit < UNITS_PER_IMAGE:
-        return (64, 96)
+    if unit == 2:
+        return (96, RUNS)
+    if unit == 3:
+        return (64, 104)
     if unit % 2 == 0:
         return SPLIT_EVEN
     return SPLIT_ODD
 
 
-SPLIT_EVEN = (48, 80)
-SPLIT_ODD = (64, 108)
+SPLIT_EVEN = (40, 64)
+SPLIT_ODD = (60, 104)
 
 
 def tile_selfattention_pa_t_kernel(
@@ -452,7 +454,6 @@ def tile_selfattention_pa_t_kernel(
         normalise_q(0)
         regroup_vector(2)
         regroup_scalar(2)
-        regroup_gpsimd(2)
         regroup_gpsimd(3)
 
         def live(unit):

from contextlib import ExitStack

import concourse.mybir as mybir
from concourse.masks import make_identity

F32 = mybir.dt.float32
BF16 = mybir.dt.bfloat16
U32 = mybir.dt.uint32
U8 = mybir.dt.uint8
FP8X4 = mybir.dt.float8_e4m3fn_x4
ACT = mybir.ActivationFunctionType
ALU = mybir.AluOpType

IMAGES = 4
CHANNELS = 512
WIDTH = 64
POSITIONS = 2048
EPS = 1e-5

P = 128
PACK = 4
UNIT = 512
PAIR = 2 * UNIT
UNITS_PER_IMAGE = POSITIONS // UNIT
PAIRS_PER_IMAGE = POSITIONS // PAIR
UNITS = IMAGES * UNITS_PER_IMAGE
WINDOWS = PAIR // 4
HALF_WIDTH = WIDTH // 2
WINDOW_ROWS = WINDOWS // HALF_WIDTH
BLOCK_ROWS = P // HALF_WIDTH
RUN = 4
RUNS = UNIT // RUN

GROUPS = 4
GROUP_Q = 0
GROUP_K = 1
POOLED_GROUPS = (1, 2, 3)

KINDS = 5
BIAS = 0
GAIN = 1
SHIFT = 2
MEAN = 3
VARIANCE = 4

NEEDS = 3
NEED_SCALE_KV = 0
NEED_Q = 1
NEED_ADDEND_KV = 2

LEAD = 3

FLOPS = 2 * IMAGES * POSITIONS * CHANNELS * GROUPS * P


def split_of(unit):
    if unit == 2:
        return (96, RUNS)
    if unit == 3:
        return (64, 104)
    if unit % 2 == 0:
        return SPLIT_EVEN
    return SPLIT_ODD


SPLIT_EVEN = (40, 64)
SPLIT_ODD = (60, 104)


def tile_selfattention_pa_t_kernel(
    tc,
    memory,
    wq, bq, bnq_s, bnq_b, bnq_m, bnq_v,
    wk, bk, bnk_s, bnk_b, bnk_m, bnk_v,
    wv, bv, bnv_s, bnv_b, bnv_m, bnv_v,
    out_q, out_k, out_v,
):
    nc = tc.nc
    with ExitStack() as ctx:
        consts = ctx.enter_context(tc.tile_pool(name="consts", bufs=1))
        raws = ctx.enter_context(tc.tile_pool(name="raws", bufs=1))
        stage = ctx.enter_context(tc.tile_pool(name="stage", bufs=2))
        work = ctx.enter_context(tc.tile_pool(name="work", bufs=2))
        rows = ctx.enter_context(tc.tile_pool(name="rows", bufs=3))
        psum_kv = ctx.enter_context(tc.psum_pool(name="psum_kv", bufs=5))
        psum_one = ctx.enter_context(tc.psum_pool(name="psum_one", bufs=1))
        ctx.enter_context(tc.manual_schedule())

        identity = consts.tile([P, P], F32)
        make_identity(nc, identity[:])
        identity_bf16 = consts.tile([P, P], BF16)
        make_identity(nc, identity_bf16[:])

        w_rows = consts.tile([P, GROUPS, CHANNELS], BF16)
        tables = []
        for need in range(NEEDS):
            table = consts.tile([P, P], BF16, name="table_%d" % need)
            nc.vector.memset(table[:], 0.0)
            tables.append(table)
        vectors_of_kind = (
            (bq, bk, bv),
            (bnq_s, bnk_s, bnv_s),
            (bnq_b, bnk_b, bnv_b),
            (bnq_m, bnk_m, bnv_m),
            (bnq_v, bnk_v, bnv_v),
        )

        def load_vector(need, kind, who):
            row = GROUPS * kind + who
            groups = 2 if who == 2 else 1
            nc.sync.dma_start(
                out=tables[need][row : row + groups, :],
                in_=vectors_of_kind[kind][who].rearrange("(g c) -> g c", g=groups),
            )

        mem = memory.rearrange("b (p j) h w -> b p j (h w)", j=PACK)
        pieces_of_pair = []
        for pair in range(UNITS // 2):
            pieces_of_pair.append([])

        def load_memory(image, first, load_width):
            raw = raws.tile([P, PACK, load_width], BF16, name="raw_%d_%d" % (image, first))
            nc.sync.dma_start(out=raw[:], in_=mem[image, :, :, first : first + load_width])
            pieces_of_pair[image * PAIRS_PER_IMAGE + first // PAIR].append((raw, (first % PAIR) // 2, load_width // 2))

        load_memory(0, 0, UNIT)
        nc.sync.dma_start(out=w_rows[:, 0, :], in_=wq)
        nc.sync.dma_start(out=w_rows[:, 1, :], in_=wk)
        nc.sync.dma_start(out=w_rows[:, 2:4, :], in_=wv.rearrange("(g c) k -> c g k", g=2))
        load_memory(0, UNIT, UNIT)
        for kind, who in ((GAIN, 2), (VARIANCE, 2), (GAIN, 1), (VARIANCE, 1)):
            load_vector(NEED_SCALE_KV, kind, who)
        for kind in (VARIANCE, GAIN, BIAS, MEAN, SHIFT):
            load_vector(NEED_Q, kind, 0)
        load_memory(0, 2 * UNIT, UNIT)
        load_memory(0, 3 * UNIT, UNIT)
        for kind in (BIAS, MEAN, SHIFT):
            for who in (1, 2):
                load_vector(NEED_ADDEND_KV, kind, who)
        for image in range(1, IMAGES):
            for first in range(0, POSITIONS, PAIR):
                load_memory(image, first, PAIR)

        mem_codes = consts.tile([P, UNITS, UNIT], U32, align_bytes=64)
        mem_scales = consts.tile([P, UNITS, UNIT], U8, align_bytes=64)
        grouped_of = {}
        sums_of = {}
        peak_of = {}
        z_q_of = {}
        z_v_of = {}
        t_q_of = {}
        t_v_of = {}
        k_of = {}
        q_rows_of = {}

        def regroup(unit, engine, first_run, end_run):
            if unit not in grouped_of:
                new_tile = stage.tile([P, UNIT, PACK], BF16, align_bytes=64, tag="grouped")
                grouped_of[unit] = new_tile
            grouped = grouped_of[unit]
            for raw, piece_first, piece_columns in pieces_of_pair[unit // 2]:
                lo = max(first_run * RUN, piece_first)
                hi = min(end_run * RUN, piece_first + piece_columns)
                if lo < hi:
                    by_parity = raw[:].rearrange("p j (n b) -> p j n b", b=2)
                    regroup_columns(
                        engine, grouped[:, lo:hi, :], by_parity[:, :, lo - piece_first : hi - piece_first, unit % 2]
                    )

        def regroup_columns(engine, dst, src):
            if engine == "vector":
                nc.vector.tensor_copy(
                    out=dst.rearrange("p (c i) j -> p c j i", i=RUN),
                    in_=src.rearrange("p j (c i) -> p c j i", i=RUN),
                )
            elif engine == "scalar":
                nc.scalar.copy(
                    out=dst.rearrange("p (c i) j -> p c j i", i=RUN),
                    in_=src.rearrange("p j (c i) -> p c j i", i=RUN),
                )
            else:
                nc.gpsimd.tensor_scalar(
                    out=dst,
                    in0=src.rearrange("p j n -> p n j"),
                    scalar1=1.0,
                    scalar2=0.0,
                    op0=ALU.mult,
                    op1=ALU.add,
                )

        def regroup_vector(unit):
            regroup(unit, "vector", 0, split_of(unit)[0])

        def regroup_scalar(unit):
            regroup(unit, "scalar", split_of(unit)[0], split_of(unit)[1])

        def regroup_gpsimd(unit):
            regroup(unit, "gpsimd", split_of(unit)[1], RUNS)

        def quantise(unit):
            nc.vector.quantize_mx(
                out=mem_codes[:, unit, :].bitcast(FP8X4),
                scales=mem_scales[:, unit, :],
                in_=grouped_of[unit][:].rearrange("p n j -> p (n j)"),
            )

        def multiply(unit, groups):
            for group in groups:
                if group == GROUP_Q:
                    acc = psum_one.tile([P, UNIT], F32, tag="acc_q")
                else:
                    acc = psum_kv.tile([P, UNIT], F32, tag="acc_kv")
                nc.tensor.matmul_mx(
                    out=acc[:],
                    lhsT=w_codes[:, group * P : (group + 1) * P].bitcast(FP8X4),
                    lhsT_scale=w_scales[:, group * P : (group + 1) * P],
                    rhs=mem_codes[:, unit, :].bitcast(FP8X4),
                    rhs_scale=mem_scales[:, unit, :],
                    start=True,
                    stop=True,
                )
                sums_of[(unit, group)] = acc

        def normalise_q(unit):
            z_q = work.tile([P, PACK, P], F32)
            nc.scalar.activation(
                out=z_q[:],
                in_=sums_of[(unit, GROUP_Q)][:].rearrange("c (r i) -> c i r", i=PACK),
                func=ACT.Identity,
                scale=inv[:, GROUP_Q : GROUP_Q + 1],
                bias=addend[:, GROUP_Q : GROUP_Q + 1],
            )
            z_q_of[unit] = z_q

        def member(unit, group, a):
            by_row = sums_of[(unit, group)][:].rearrange("c (hh a ww) -> c a hh ww", a=2, ww=HALF_WIDTH)
            return by_row[:, a]

        def by_window_row(flat):
            return flat.rearrange("c (hh ww) -> c hh ww", ww=HALF_WIDTH)

        def peak_view(pair, group):
            return by_window_row(peak_of[pair][:, group - 1, :])

        def start_windows(unit, groups):
            pair = unit // 2
            if pair not in peak_of:
                peak = work.tile([P, len(POOLED_GROUPS), WINDOWS], F32)
                peak_of[pair] = peak
            for group in groups:
                nc.scalar.activation(
                    out=peak_view(pair, group),
                    in_=member(unit, group, 0),
                    func=ACT.Copy,
                    scale=inv[:, group : group + 1],
                )

        def fold_windows(unit):
            pair = unit // 2
            image = pair // PAIRS_PER_IMAGE
            pair_in_image = pair % PAIRS_PER_IMAGE
            odd = unit % 2 == 1
            if odd:
                if pair_in_image == 0:
                    k_image = work.tile([P, PAIRS_PER_IMAGE, WINDOWS], F32)
                    k_of[image] = k_image
                z_v = work.tile([P, 2, WINDOWS], F32)
                z_v_of[pair] = z_v
                finished = (k_of[image][:, pair_in_image, :], z_v[:, 0, :], z_v[:, 1, :])
            every_row = slice(0, WINDOW_ROWS)
            turns = []
            if odd:
                turns.extend([(group, 0, every_row) for group in POOLED_GROUPS])
            if unit < UNITS - 1:
                turns.extend([(group, 1, every_row) for group in POOLED_GROUPS])
            else:
                for first_row in range(0, WINDOW_ROWS, BLOCK_ROWS):
                    turns.extend([(group, 1, slice(first_row, first_row + BLOCK_ROWS)) for group in POOLED_GROUPS[1:]])
                turns.append((GROUP_K, 1, every_row))
            for group, a, window_rows in turns:
                if odd and a == 1:
                    target = by_window_row(finished[group - 1])
                else:
                    target = peak_view(pair, group)
                nc.vector.scalar_tensor_tensor(
                    out=target[:, window_rows, :],
                    in0=member(unit, group, a)[:, window_rows, :],
                    scalar=inv[:, group : group + 1],
                    in1=peak_view(pair, group)[:, window_rows, :],
                    op0=ALU.mult,
                    op1=ALU.max,
                )
            if image == IMAGES - 1:
                first_pair = pair_in_image
            else:
                first_pair = 0
            if odd and (image == IMAGES - 1 or pair_in_image == PAIRS_PER_IMAGE - 1):
                k_rows = work.tile([P, (pair_in_image + 1 - first_pair) * WINDOWS], F32)
                nc.vector.tensor_scalar_add(
                    out=k_rows[:],
                    in0=k_of[image][:, first_pair : pair_in_image + 1, :].rearrange("c u n -> c (u n)"),
                    scalar1=addend[:, GROUP_K : GROUP_K + 1],
                )
                nc.sync.dma_start(
                    out=out_k[image, :, first_pair * WINDOWS : (pair_in_image + 1) * WINDOWS], in_=k_rows[:]
                )

        def transpose_q(unit):
            t_q = psum_one.tile([P, PACK, P], F32, tag="t_q")
            for i in range(PACK):
                nc.tensor.transpose(out=t_q[:, i, :], in_=z_q_of[unit][:, i, :], identity=identity[:])
            t_q_of[unit] = t_q

        def transpose_v(pair, blocks):
            if len(blocks) == 2:
                t_v = psum_one.tile([P, 2, 2, P], F32, tag="t_v")
            else:
                t_v = psum_kv.tile([P, 1, 2, P], F32, tag="acc_kv")
            for slot, block in enumerate(blocks):
                for half in range(2):
                    group = POOLED_GROUPS[1 + half]
                    nc.tensor.matmul(
                        out=t_v[:, slot, half, :],
                        lhsT=addend[:, group : group + 1].to_broadcast([P, P]),
                        rhs=identity[:],
                        is_transpose=True,
                        start=True,
                        stop=False,
                    )
                    nc.tensor.matmul(
                        out=t_v[:, slot, half, :],
                        lhsT=z_v_of[pair][:, half, block * P : (block + 1) * P],
                        rhs=identity[:],
                        is_transpose=True,
                        start=False,
                        stop=True,
                    )
            t_v_of[(pair, blocks)] = t_v

        def store_q(unit):
            pair = unit // 2
            if pair not in q_rows_of:
                q_rows = rows.tile([P, PACK, 2, P], F32)
                q_rows_of[pair] = q_rows
            nc.scalar.copy(out=q_rows_of[pair][:, :, unit % 2, :], in_=t_q_of[unit][:])
            first = (pair % PAIRS_PER_IMAGE) * PAIR
            q_of_pair = out_q[pair // PAIRS_PER_IMAGE, first : first + PAIR, :].rearrange(
                "(r i b) c -> r i b c", i=PACK, b=2
            )
            if pair == UNITS // 2 - 1:
                nc.sync.dma_start(out=q_of_pair[:, :, unit % 2, :], in_=q_rows_of[pair][:, :, unit % 2, :])
            elif unit % 2 == 1:
                nc.sync.dma_start(out=q_of_pair, in_=q_rows_of[pair][:])

        def store_v(pair, blocks, engine):
            v_rows = rows.tile([P, len(blocks), 2, P], F32)
            if engine == "vector":
                nc.vector.tensor_copy(out=v_rows[:], in_=t_v_of[(pair, blocks)][:])
            else:
                nc.scalar.copy(out=v_rows[:], in_=t_v_of[(pair, blocks)][:])
            first = (pair % PAIRS_PER_IMAGE) * WINDOWS + blocks[0] * P
            nc.sync.dma_start(
                out=out_v[pair // PAIRS_PER_IMAGE, first : first + len(blocks) * P, :].rearrange(
                    "(e n) (h c) -> n e h c", e=len(blocks), h=2
                ),
                in_=v_rows[:],
            )

        warm = consts.tile([P, 2], F32)
        nc.vector.memset(warm[:], 1.0)
        nc.scalar.sqrt(out=warm[:, 1:2], in_=warm[:, 0:1])

        regroup(0, "vector", 0, RUNS // 2)
        regroup(1, "scalar", 0, RUNS // 2)

        w_grouped = consts.tile([P, GROUPS * P * PACK], BF16, align_bytes=64)
        w_grouped_words = w_grouped[:].bitcast(F32).rearrange("p (g c e) -> p g c e", g=GROUPS, e=2)
        for half in range(2):
            w_t = psum_kv.tile([P, 2, 2, P], F32, tag="acc_kv")
            for g in range(2):
                words = w_rows[:, 2 * half + g, :].bitcast(F32).rearrange("c (p e) -> c e p", e=2)
                for e in range(2):
                    nc.tensor.transpose(out=w_t[:, g, e, :], in_=words[:, e, :], identity=identity[:])
            if half == 0:
                nc.vector.tensor_copy(
                    out=w_grouped_words[:, 0:2, :, :], in_=w_t[:].rearrange("p g e c -> p g c e")
                )
            else:
                nc.scalar.copy(out=w_grouped_words[:, 2:4, :, :], in_=w_t[:].rearrange("p g e c -> p g c e"))
        w_codes = consts.tile([P, GROUPS * P], U32, align_bytes=64)
        w_scales = consts.tile([P, GROUPS * P], U8, align_bytes=64)

        def quantise_weights(half):
            columns = slice(half * 2 * P, (half + 1) * 2 * P)
            nc.vector.quantize_mx(
                out=w_codes[:, columns].bitcast(FP8X4),
                scales=w_scales[:, columns],
                in_=w_grouped[:, half * 2 * P * PACK : (half + 1) * 2 * P * PACK],
            )

        quantise_weights(0)
        regroup(0, "vector", RUNS // 2, RUNS)
        regroup(1, "scalar", RUNS // 2, RUNS)
        quantise_weights(1)
        quantise(0)

        inv = consts.tile([P, GROUPS], F32)
        addend = consts.tile([P, GROUPS], F32)
        deviation = consts.tile([P, GROUPS], F32)
        inv_deviation = consts.tile([P, GROUPS], F32)
        centred = consts.tile([P, GROUPS], F32)
        scaled = consts.tile([P, GROUPS], F32)
        own_of = {}

        def fetch_table(need, tag, groups, with_variance):
            table_t = psum_one.tile([P, P], BF16, tag=tag)
            nc.tensor.transpose(out=table_t[:], in_=tables[need][:], identity=identity_bf16[:])
            values = table_t[:, 0 : KINDS * GROUPS].rearrange("p (k g) -> p k g", g=GROUPS)
            if with_variance:
                nc.scalar.activation(
                    out=deviation[:, groups], in_=values[:, VARIANCE, groups], func=ACT.Sqrt, bias=EPS
                )
            own = consts.tile([P, KINDS, GROUPS], F32, name="own_%d" % need)
            nc.scalar.copy(out=own[:, BIAS : MEAN + 1, :], in_=values[:, BIAS : MEAN + 1, :])
            own_of[need] = own

        def invert(groups):
            nc.vector.reciprocal(out=inv_deviation[:, groups], in_=deviation[:, groups])

        def make_inv(need, groups):
            nc.gpsimd.tensor_mul(out=inv[:, groups], in0=own_of[need][:, GAIN, groups], in1=inv_deviation[:, groups])

        def centre(need, groups):
            own = own_of[need]
            nc.gpsimd.tensor_sub(out=centred[:, groups], in0=own[:, BIAS, groups], in1=own[:, MEAN, groups])

        def make_addend(need, groups):
            nc.gpsimd.tensor_mul(out=scaled[:, groups], in0=centred[:, groups], in1=inv[:, groups])
            nc.gpsimd.tensor_add(out=addend[:, groups], in0=scaled[:, groups], in1=own_of[need][:, SHIFT, groups])

        pooled = slice(GROUP_K, GROUPS)
        only_q = slice(GROUP_Q, GROUP_Q + 1)
        fetch_table(NEED_SCALE_KV, "t_v", pooled, True)
        invert(pooled)
        make_inv(NEED_SCALE_KV, pooled)
        fetch_table(NEED_Q, "t_q", only_q, True)
        centre(NEED_Q, only_q)
        multiply(0, range(GROUPS))
        start_windows(0, POOLED_GROUPS)
        quantise(1)
        invert(only_q)
        make_inv(NEED_Q, only_q)
        make_addend(NEED_Q, only_q)
        normalise_q(0)
        regroup_vector(2)
        regroup_scalar(2)
        regroup_gpsimd(3)

        def live(unit):
            return 0 <= unit < UNITS

        both = (0, 1)
        for step in range(UNITS + 1):
            if 4 <= step <= UNITS - 2 and step % 2 == 0:
                store_v((step - 4) // 2, both, "scalar")
            if live(step + 1):
                multiply(step + 1, range(GROUPS))
            if live(step):
                transpose_q(step)
            if 3 <= step < UNITS - 2 and step % 2 == 1:
                transpose_v((step - 3) // 2, both)
            if step == UNITS - 2:
                transpose_v(step // 2 - 1, both)
            if step == UNITS:
                transpose_v(step // 2 - 1, (0,))
                transpose_v(step // 2 - 1, (1,))
            if live(step + 1):
                if (step + 1) % 2 == 0:
                    start_windows(step + 1, POOLED_GROUPS[:2])
                normalise_q(step + 1)
                if (step + 1) % 2 == 0:
                    start_windows(step + 1, POOLED_GROUPS[2:])
            if live(step):
                fold_windows(step)
            if live(step + LEAD - 1):
                quantise(step + LEAD - 1)
            if live(step + LEAD):
                regroup_vector(step + LEAD)
                regroup_scalar(step + LEAD)
            if live(step + LEAD + 1):
                regroup_gpsimd(step + LEAD + 1)
            if step == 1:
                fetch_table(NEED_ADDEND_KV, "t_v", pooled, False)
                centre(NEED_ADDEND_KV, pooled)
                make_addend(NEED_ADDEND_KV, pooled)
            if live(step):
                store_q(step)
            if step == UNITS - 2:
                store_v(step // 2 - 1, both, "scalar")
            if step == UNITS:
                store_v(step // 2 - 1, (0,), "vector")
                store_v(step // 2 - 1, (1,), "scalar")
